import numpy as np
import ml_dtypes


def mxq(x, axis, fmt="e4m3"):
    dtype, down = {"e4m3": (ml_dtypes.float8_e4m3fn, 7), "e5m2": (ml_dtypes.float8_e5m2, 14)}[fmt]
    v = np.moveaxis(np.asarray(x, np.float32).astype(ml_dtypes.bfloat16).astype(np.float64), axis, -1)
    blocks = v.reshape(v.shape[:-1] + (-1, 32))
    amax = np.abs(blocks).max(-1, keepdims=True)
    byte = np.maximum(np.where(amax > 0, np.frexp(amax)[1] - 1 + 127, 0) - down, 1)
    scale = np.exp2(byte - 127.0)
    codes = (blocks / scale).astype(np.float32).astype(dtype).astype(np.float64)
    return np.moveaxis((codes * scale).reshape(v.shape), -1, axis)


WIDE = False


def mx_kscale(k):
    if not WIDE:
        return np.ones(k)
    levels = np.array([10, -10, 5, -5, 0])
    a = np.random.permutation(np.resize(levels, k // 512 * 4)).reshape(k // 512, 4)
    idx = np.arange(k)
    return np.exp2(a[idx // 512, idx % 128 // 32])


BF16 = ml_dtypes.bfloat16


def bf(x):
    return np.asarray(x, np.float32).astype(BF16)


def f64(x):
    return np.asarray(x).astype(np.float64)


OBS, H1, H2, ACT, B = 64, 20, 512, 128, 128
G = 4 * H2


def sigmoid(v):
    return 1.0 / (1.0 + np.exp(-v))


def setup_inputs():
    s = mx_kscale(H2)
    return {
        "h_fc2": bf(np.maximum(np.random.standard_normal((B, H2)), 0.0) * s),
        "hx": bf(np.random.standard_normal((B, H2)) * 0.5 * s),
        "cx": bf(np.random.standard_normal((B, H2)) * 0.8),
        "w_ih": bf(np.random.standard_normal((G, H2)) / np.sqrt(H2) / s),
        "w_hh": bf(np.random.standard_normal((G, H2)) / np.sqrt(H2) / s),
        "b_ih": bf(np.random.standard_normal(G) * 0.2),
        "b_hh": bf(np.random.standard_normal(G) * 0.2),
        "fc3_w": bf(np.random.standard_normal((ACT, H2)) * 3.0 / np.sqrt(H2)),
        "fc3_b": bf(np.random.standard_normal(ACT) * 0.3),
    }


def reference(h_fc2, hx, cx, w_ih, w_hh, b_ih, b_hh, fc3_w, fc3_b):
    gates = ((mxq(f64(h_fc2), 1, "e4m3") @ mxq(f64(w_ih), 1, "e4m3").T) + f64(b_ih)
             + (mxq(f64(hx), 1, "e4m3") @ mxq(f64(w_hh), 1, "e4m3").T) + f64(b_hh))
    i, f, g, o = np.split(gates, 4, axis=-1)
    i, f, o = sigmoid(i), sigmoid(f), sigmoid(o)
    g = np.tanh(g)
    cx_new = f * f64(cx) + i * g
    hx_new = o * np.tanh(cx_new)
    act = np.tanh((mxq(hx_new, 1, "e4m3") @ mxq(f64(fc3_w), 1, "e4m3").T) + f64(fc3_b))
    return act, hx_new, cx_new

@@ -1,0 +1,216 @@
+from contextlib import ExitStack
+
+import concourse.mybir as mybir
+from concourse.masks import make_identity
+
+BF16 = mybir.dt.bfloat16
+F32 = mybir.dt.float32
+U32 = mybir.dt.uint32
+U8 = mybir.dt.uint8
+FP8X4 = mybir.dt.float8_e4m3fn_x4
+FUNC = mybir.ActivationFunctionType
+
+P = 128
+BATCH = 128
+K = 512
+HIDDEN = 512
+BLOCKS = HIDDEN // P
+GATES = 4
+ACTIONS = 128
+PACK = 4
+SLOTS = 4
+
+FLOPS = 2 * BATCH * K * (2 * GATES * HIDDEN + ACTIONS)
+
+
+def transpose_four(nc, bank, words, ident):
+    for t in range(SLOTS):
+        nc.tensor.transpose(bank[:, t, :], words[:, t * P : (t + 1) * P], ident)
+
+
+def copy_pairs_side_by_side(copy, grouped_words, bank):
+    copy(
+        out=grouped_words.rearrange("q (o c u) -> q o c u", o=2, u=2),
+        in_=bank[:].rearrange("q (o u) c -> q o c u", u=2),
+    )
+
+
+def tile_actor_pa_s_kernel(
+    tc, h_fc2, hx, cx, w_ih, w_hh, b_ih, b_hh, fc3_w, fc3_b, out_0, out_1, out_2
+):
+    nc = tc.nc
+    with ExitStack() as ctx:
+        consts = ctx.enter_context(tc.tile_pool(name="consts", bufs=1))
+        raw = ctx.enter_context(tc.tile_pool(name="raw", bufs=1))
+        regroup = ctx.enter_context(tc.tile_pool(name="regroup", bufs=3))
+        mx = ctx.enter_context(tc.tile_pool(name="mx", bufs=1))
+        work = ctx.enter_context(tc.tile_pool(name="work", bufs=1))
+        weight_banks = ctx.enter_context(tc.psum_pool(name="weight_banks", bufs=4))
+        gate_banks = ctx.enter_context(tc.psum_pool(name="gate_banks", bufs=2))
+        other_banks = ctx.enter_context(tc.psum_pool(name="other_banks", bufs=2))
+
+        x_raw = raw.tile([P, 2 * K], BF16)
+        nc.sync.dma_start(out=x_raw[:, 0:K], in_=h_fc2)
+        nc.sync.dma_start(out=x_raw[:, K : 2 * K], in_=hx)
+
+        w_raw = {}
+
+        def load_gate_weights(g):
+            for s, w in enumerate((w_ih, w_hh)):
+                w_raw[s, g] = raw.tile([P, BLOCKS * K], BF16, name="w_raw_%d_%d" % (s, g))
+                nc.sync.dma_start(
+                    out=w_raw[s, g][:],
+                    in_=w[g * HIDDEN : (g + 1) * HIDDEN, :].rearrange("(p j) k -> p (j k)", j=BLOCKS),
+                )
+
+        load_gate_weights(0)
+        b_raw = raw.tile([P, 2 * GATES * BLOCKS], BF16)
+        for s, b in enumerate((b_ih, b_hh)):
+            nc.sync.dma_start(
+                out=b_raw[:, s * GATES * BLOCKS : (s + 1) * GATES * BLOCKS].rearrange(
+                    "p (g j) -> p g j", j=BLOCKS
+                ),
+                in_=b.rearrange("(g p j) -> p g j", g=GATES, j=BLOCKS),
+            )
+        cx_raw = raw.tile([P, HIDDEN], BF16)
+        nc.sync.dma_start(out=cx_raw[:], in_=cx)
+        load_gate_weights(1)
+        fc3_raw = raw.tile([P, K], BF16)
+        nc.sync.dma_start(out=fc3_raw[:], in_=fc3_w)
+        fc3_b_rows = raw.tile([P, ACTIONS], BF16)
+        nc.sync.dma_start(out=fc3_b_rows[:], in_=fc3_b.partition_broadcast(P))
+        load_gate_weights(2)
+        load_gate_weights(3)
+
+        ident = consts.tile([P, P], F32)
+        make_identity(nc, ident[:])
+        warm = consts.tile([P, 1], F32)
+        nc.vector.memset(warm[:], 0.0)
+        nc.scalar.activation(out=warm[:], in_=warm[:], func=FUNC.Sigmoid)
+
+        x_bank = other_banks.tile([P, SLOTS, P], F32, tag="other")
+        transpose_four(nc, x_bank, x_raw[:].bitcast(F32), ident[:])
+        x_grouped = work.tile([P, 2 * BATCH * PACK], BF16, align_bytes=64)
+        copy_pairs_side_by_side(nc.vector.tensor_copy, x_grouped[:].bitcast(F32), x_bank)
+        x_codes = mx.tile([P, 2 * BATCH], U32, align_bytes=64)
+        x_scales = mx.tile([P, 2 * BATCH], U8, align_bytes=64)
+        nc.vector.quantize_mx(out=x_codes[:].bitcast(FP8X4), scales=x_scales[:], in_=x_grouped[:])
+
+        bias = work.tile([P, GATES * BLOCKS], F32)
+        nc.vector.tensor_add(
+            out=bias[:], in0=b_raw[:, 0 : GATES * BLOCKS], in1=b_raw[:, GATES * BLOCKS :]
+        )
+
+        cx_blocks = work.tile([P, BLOCKS, P], F32)
+        nc.vector.tensor_copy(out=cx_blocks[:], in_=cx_raw[:].rearrange("b (p j) -> b j p", j=BLOCKS))
+        cx_t = other_banks.tile([P, BLOCKS, BATCH], F32, tag="other")
+        for j in range(BLOCKS):
+            nc.tensor.transpose(cx_t[:, j, :], cx_blocks[:, j, :], ident[:])
+
+        fc3_bank = other_banks.tile([P, 2, P], F32, tag="other")
+        fc3_words = fc3_raw[:].bitcast(F32).rearrange("a (p u) -> a u p", u=2)
+        for u in range(2):
+            nc.tensor.transpose(fc3_bank[:, u, :], fc3_words[:, u, :], ident[:])
+        fc3_grouped = work.tile([P, ACTIONS * PACK], BF16, align_bytes=64)
+        nc.vector.tensor_copy(
+            out=fc3_grouped[:].bitcast(F32).rearrange("p (a u) -> p a u", u=2),
+            in_=fc3_bank[:].rearrange("p u a -> p a u"),
+        )
+        fc3_codes = mx.tile([P, ACTIONS], U32, align_bytes=64)
+        fc3_scales = mx.tile([P, ACTIONS], U8, align_bytes=64)
+        nc.vector.quantize_mx(
+            out=fc3_codes[:].bitcast(FP8X4), scales=fc3_scales[:], in_=fc3_grouped[:]
+        )
+
+        def store_batch_major(value_t, dram_out, label):
+            bank = other_banks.tile([P, BLOCKS, P], F32, tag="other", name="bank_" + label)
+            for j in range(BLOCKS):
+                nc.tensor.transpose(bank[:, j, :], value_t[:, j, :], ident[:])
+            rows = work.tile([P, HIDDEN], F32, name="rows_" + label)
+            nc.scalar.copy(
+                out=rows[:].rearrange("b (p j) -> b p j", j=BLOCKS),
+                in_=bank[:].rearrange("b j p -> b p j"),
+            )
+            nc.sync.dma_start(out=dram_out, in_=rows[:])
+
+        gate = {}
+        for g in range(GATES):
+            w_codes = {}
+            w_scales = {}
+            for s in range(2):
+                w_words = w_raw[s, g][:].bitcast(F32)
+                grouped = regroup.tile([P, BLOCKS * P * PACK], BF16, align_bytes=64, tag="grouped")
+                grouped_words = grouped[:].bitcast(F32)
+                for half in range(2):
+                    bank = weight_banks.tile([P, SLOTS, P], F32, tag="weights")
+                    cols = slice(half * SLOTS * P, (half + 1) * SLOTS * P)
+                    transpose_four(nc, bank, w_words[:, cols], ident[:])
+                    copy = nc.vector.tensor_copy if (s == 1 and half == 1) else nc.scalar.copy
+                    copy_pairs_side_by_side(copy, grouped_words[:, cols], bank)
+                w_codes[s] = mx.tile([P, BLOCKS * P], U32, align_bytes=64, name="w_codes_%d_%d" % (s, g))
+                w_scales[s] = mx.tile([P, BLOCKS * P], U8, align_bytes=64, name="w_scales_%d_%d" % (s, g))
+                nc.vector.quantize_mx(
+                    out=w_codes[s][:].bitcast(FP8X4), scales=w_scales[s][:], in_=grouped[:]
+                )
+
+            gate_bank = gate_banks.tile([P, BLOCKS, BATCH], F32, tag="gate")
+            gate[g] = work.tile([P, BLOCKS, BATCH], F32, name="gate_%d" % g)
+            for j in range(BLOCKS):
+                for s in range(2):
+                    nc.tensor.matmul_mx(
+                        out=gate_bank[:, j, :],
+                        lhsT=w_codes[s][:, j * P : (j + 1) * P].bitcast(FP8X4),
+                        lhsT_scale=w_scales[s][:, j * P : (j + 1) * P],
+                        rhs=x_codes[:, s * BATCH : (s + 1) * BATCH].bitcast(FP8X4),
+                        rhs_scale=x_scales[:, s * BATCH : (s + 1) * BATCH],
+                        start=(s == 0),
+                        stop=(s == 1),
+                    )
+            for j in range(BLOCKS):
+                nc.scalar.activation(
+                    out=gate[g][:, j, :],
+                    in_=gate_bank[:, j, :],
+                    func=FUNC.Tanh if g == 2 else FUNC.Sigmoid,
+                    bias=bias[:, g * BLOCKS + j : g * BLOCKS + j + 1],
+                )
+
+            if g == 1:
+                kept = work.tile([P, BLOCKS, BATCH], F32)
+                nc.vector.tensor_mul(out=kept[:], in0=gate[1][:], in1=cx_t[:])
+            if g == 2:
+                fresh = work.tile([P, BLOCKS, BATCH], F32)
+                nc.vector.tensor_mul(out=fresh[:], in0=gate[0][:], in1=gate[2][:])
+                cx_new = work.tile([P, BLOCKS, BATCH], F32)
+                nc.vector.tensor_add(out=cx_new[:], in0=kept[:], in1=fresh[:])
+                tanh_c = work.tile([P, BLOCKS, BATCH], F32)
+                nc.scalar.activation(out=tanh_c[:], in_=cx_new[:], func=FUNC.Tanh)
+                store_batch_major(cx_new, out_2, "cx")
+
+        hx_new = work.tile([P, BLOCKS, BATCH], F32)
+        nc.vector.tensor_mul(out=hx_new[:], in0=gate[3][:], in1=tanh_c[:])
+
+        hx_grouped = work.tile([P, BATCH, PACK], BF16, align_bytes=64)
+        nc.vector.tensor_copy(out=hx_grouped[:], in_=hx_new[:].rearrange("p j b -> p b j"))
+        hx_codes = mx.tile([P, BATCH], U32, align_bytes=64)
+        hx_scales = mx.tile([P, BATCH], U8, align_bytes=64)
+        nc.vector.quantize_mx(
+            out=hx_codes[:].bitcast(FP8X4),
+            scales=hx_scales[:],
+            in_=hx_grouped[:].rearrange("p b j -> p (b j)"),
+        )
+        store_batch_major(hx_new, out_1, "hx")
+
+        act_bank = other_banks.tile([P, ACTIONS], F32, tag="other")
+        nc.tensor.matmul_mx(
+            out=act_bank[:],
+            lhsT=hx_codes[:].bitcast(FP8X4),
+            lhsT_scale=hx_scales[:],
+            rhs=fc3_codes[:].bitcast(FP8X4),
+            rhs_scale=fc3_scales[:],
+            start=True,
+            stop=True,
+        )
+        act = work.tile([P, ACTIONS], F32)
+        nc.vector.tensor_add(out=act[:], in0=act_bank[:], in1=fc3_b_rows[:])
+        nc.scalar.activation(out=act[:], in_=act[:], func=FUNC.Tanh)
+        nc.sync.dma_start(out=out_0, in_=act[:])

@@ -15,10 +15,13 @@ BATCH = 128
 K = 512
 HIDDEN = 512
 BLOCKS = HIDDEN // P
+GATE_I, GATE_F, GATE_G, GATE_O = 0, 1, 2, 3
 GATES = 4
 ACTIONS = 128
 PACK = 4
 SLOTS = 4
+HALVES = 2
+HALF_BLOCKS = BLOCKS // HALVES
 
 FLOPS = 2 * BATCH * K * (2 * GATES * HIDDEN + ACTIONS)
 
@@ -28,9 +31,9 @@ def transpose_four(nc, bank, words, ident):
         nc.tensor.transpose(bank[:, t, :], words[:, t * P : (t + 1) * P], ident)
 
 
-def copy_pairs_side_by_side(copy, grouped_words, bank):
+def copy_pairs_side_by_side(copy, grouped, bank):
     copy(
-        out=grouped_words.rearrange("q (o c u) -> q o c u", o=2, u=2),
+        out=grouped[:].bitcast(F32).rearrange("q (o c u) -> q o c u", o=2, u=2),
         in_=bank[:].rearrange("q (o u) c -> q o c u", u=2),
     )
 
@@ -40,30 +43,31 @@ def tile_actor_pa_s_kernel(
 ):
     nc = tc.nc
     with ExitStack() as ctx:
+        ctx.enter_context(tc.manual_schedule())
         consts = ctx.enter_context(tc.tile_pool(name="consts", bufs=1))
         raw = ctx.enter_context(tc.tile_pool(name="raw", bufs=1))
-        regroup = ctx.enter_context(tc.tile_pool(name="regroup", bufs=3))
+        regroup = ctx.enter_context(tc.tile_pool(name="regroup", bufs=4))
         mx = ctx.enter_context(tc.tile_pool(name="mx", bufs=1))
         work = ctx.enter_context(tc.tile_pool(name="work", bufs=1))
         weight_banks = ctx.enter_context(tc.psum_pool(name="weight_banks", bufs=4))
         gate_banks = ctx.enter_context(tc.psum_pool(name="gate_banks", bufs=2))
         other_banks = ctx.enter_context(tc.psum_pool(name="other_banks", bufs=2))
 
+        w_raw = {}
+
+        def load_weights(s, g):
+            w = (w_ih, w_hh)[s]
+            w_raw[s, g] = raw.tile([P, BLOCKS * K], BF16, name="w_raw_%d_%d" % (s, g))
+            nc.sync.dma_start(
+                out=w_raw[s, g][:],
+                in_=w[g * HIDDEN : (g + 1) * HIDDEN, :].rearrange("(p j) k -> p (j k)", j=BLOCKS),
+            )
+
+        load_weights(0, 0)
         x_raw = raw.tile([P, 2 * K], BF16)
         nc.sync.dma_start(out=x_raw[:, 0:K], in_=h_fc2)
         nc.sync.dma_start(out=x_raw[:, K : 2 * K], in_=hx)
-
-        w_raw = {}
-
-        def load_gate_weights(g):
-            for s, w in enumerate((w_ih, w_hh)):
-                w_raw[s, g] = raw.tile([P, BLOCKS * K], BF16, name="w_raw_%d_%d" % (s, g))
-                nc.sync.dma_start(
-                    out=w_raw[s, g][:],
-                    in_=w[g * HIDDEN : (g + 1) * HIDDEN, :].rearrange("(p j) k -> p (j k)", j=BLOCKS),
-                )
-
-        load_gate_weights(0)
+        load_weights(1, 0)
         b_raw = raw.tile([P, 2 * GATES * BLOCKS], BF16)
         for s, b in enumerate((b_ih, b_hh)):
             nc.sync.dma_start(
@@ -74,53 +78,102 @@ def tile_actor_pa_s_kernel(
             )
         cx_raw = raw.tile([P, HIDDEN], BF16)
         nc.sync.dma_start(out=cx_raw[:], in_=cx)
-        load_gate_weights(1)
+        load_weights(0, 1)
         fc3_raw = raw.tile([P, K], BF16)
         nc.sync.dma_start(out=fc3_raw[:], in_=fc3_w)
         fc3_b_rows = raw.tile([P, ACTIONS], BF16)
         nc.sync.dma_start(out=fc3_b_rows[:], in_=fc3_b.partition_broadcast(P))
-        load_gate_weights(2)
-        load_gate_weights(3)
+        load_weights(1, 1)
+        for g in (GATE_G, GATE_O):
+            for s in range(2):
+                load_weights(s, g)
 
         ident = consts.tile([P, P], F32)
         make_identity(nc, ident[:])
+        ident_bf16 = consts.tile([P, P], BF16)
+        make_identity(nc, ident_bf16[:])
         warm = consts.tile([P, 1], F32)
         nc.vector.memset(warm[:], 0.0)
         nc.scalar.activation(out=warm[:], in_=warm[:], func=FUNC.Sigmoid)
 
-        x_bank = other_banks.tile([P, SLOTS, P], F32, tag="other")
-        transpose_four(nc, x_bank, x_raw[:].bitcast(F32), ident[:])
-        x_grouped = work.tile([P, 2 * BATCH * PACK], BF16, align_bytes=64)
-        copy_pairs_side_by_side(nc.vector.tensor_copy, x_grouped[:].bitcast(F32), x_bank)
-        x_codes = mx.tile([P, 2 * BATCH], U32, align_bytes=64)
-        x_scales = mx.tile([P, 2 * BATCH], U8, align_bytes=64)
-        nc.vector.quantize_mx(out=x_codes[:].bitcast(FP8X4), scales=x_scales[:], in_=x_grouped[:])
+        banks = {}
+        grouped = {}
+        w_codes = {}
+        w_scales = {}
 
-        bias = work.tile([P, GATES * BLOCKS], F32)
-        nc.vector.tensor_add(
-            out=bias[:], in0=b_raw[:, 0 : GATES * BLOCKS], in1=b_raw[:, GATES * BLOCKS :]
-        )
+        def transpose_weights(s, g):
+            w_words = w_raw[s, g][:].bitcast(F32)
+            for half in range(HALVES):
+                banks[half] = weight_banks.tile([P, SLOTS, P], F32, tag="weights", name="bank_%d" % half)
+                transpose_four(nc, banks[half], w_words[:, half * SLOTS * P : (half + 1) * SLOTS * P], ident[:])
 
-        cx_blocks = work.tile([P, BLOCKS, P], F32)
-        nc.vector.tensor_copy(out=cx_blocks[:], in_=cx_raw[:].rearrange("b (p j) -> b j p", j=BLOCKS))
-        cx_t = other_banks.tile([P, BLOCKS, BATCH], F32, tag="other")
-        for j in range(BLOCKS):
-            nc.tensor.transpose(cx_t[:, j, :], cx_blocks[:, j, :], ident[:])
+        def empty_banks(s):
+            for half in range(HALVES):
+                grouped[half] = regroup.tile(
+                    [P, HALF_BLOCKS * P * PACK], BF16, align_bytes=64, tag="grouped", name="grouped_%d" % half
+                )
+                copy = nc.vector.tensor_copy if (s == 0 and half == 1) else nc.scalar.copy
+                copy_pairs_side_by_side(copy, grouped[half], banks[half])
 
-        fc3_bank = other_banks.tile([P, 2, P], F32, tag="other")
-        fc3_words = fc3_raw[:].bitcast(F32).rearrange("a (p u) -> a u p", u=2)
-        for u in range(2):
-            nc.tensor.transpose(fc3_bank[:, u, :], fc3_words[:, u, :], ident[:])
-        fc3_grouped = work.tile([P, ACTIONS * PACK], BF16, align_bytes=64)
-        nc.vector.tensor_copy(
-            out=fc3_grouped[:].bitcast(F32).rearrange("p (a u) -> p a u", u=2),
-            in_=fc3_bank[:].rearrange("p u a -> p a u"),
-        )
-        fc3_codes = mx.tile([P, ACTIONS], U32, align_bytes=64)
-        fc3_scales = mx.tile([P, ACTIONS], U8, align_bytes=64)
-        nc.vector.quantize_mx(
-            out=fc3_codes[:].bitcast(FP8X4), scales=fc3_scales[:], in_=fc3_grouped[:]
-        )
+        def quantise_weights(s, g):
+            w_codes[s, g] = mx.tile([P, BLOCKS * P], U32, align_bytes=64, name="w_codes_%d_%d" % (s, g))
+            w_scales[s, g] = mx.tile([P, BLOCKS * P], U8, align_bytes=64, name="w_scales_%d_%d" % (s, g))
+            for half in range(HALVES):
+                cols = slice(half * HALF_BLOCKS * P, (half + 1) * HALF_BLOCKS * P)
+                nc.vector.quantize_mx(
+                    out=w_codes[s, g][:, cols].bitcast(FP8X4),
+                    scales=w_scales[s, g][:, cols],
+                    in_=grouped[half][:],
+                )
+
+        gate = {}
+
+        def multiply_and_activate(g):
+            gate[g] = work.tile([P, BLOCKS, BATCH], F32, name="gate_%d" % g)
+            for half in range(HALVES):
+                gate_bank = gate_banks.tile([P, HALF_BLOCKS, BATCH], F32, tag="gate")
+                for i in range(HALF_BLOCKS):
+                    j = half * HALF_BLOCKS + i
+                    for s in range(2):
+                        nc.tensor.matmul_mx(
+                            out=gate_bank[:, i, :],
+                            lhsT=w_codes[s, g][:, j * P : (j + 1) * P].bitcast(FP8X4),
+                            lhsT_scale=w_scales[s, g][:, j * P : (j + 1) * P],
+                            rhs=x_codes[:, s * BATCH : (s + 1) * BATCH].bitcast(FP8X4),
+                            rhs_scale=x_scales[:, s * BATCH : (s + 1) * BATCH],
+                            start=(s == 0),
+                            stop=(s == 1),
+                        )
+                for i in range(HALF_BLOCKS):
+                    j = half * HALF_BLOCKS + i
+                    nc.scalar.activation(
+                        out=gate[g][:, j, :],
+                        in_=gate_bank[:, i, :],
+                        func=FUNC.Tanh if g == GATE_G else FUNC.Sigmoid,
+                        bias=bias[:, g * BLOCKS + j : g * BLOCKS + j + 1],
+                    )
+
+        kept = work.tile([P, BLOCKS, BATCH], F32)
+        fresh = work.tile([P, BLOCKS, BATCH], F32)
+        cx_new = work.tile([P, BLOCKS, BATCH], F32)
+        tanh_c = work.tile([P, BLOCKS, BATCH], F32)
+        hx_new = work.tile([P, BLOCKS, BATCH], F32)
+        hx_grouped = work.tile([P, BATCH, PACK], BF16, align_bytes=64)
+
+        def combine(g):
+            for half in range(HALVES):
+                js = slice(half * HALF_BLOCKS, (half + 1) * HALF_BLOCKS)
+                if g == GATE_F:
+                    nc.vector.tensor_mul(out=kept[:, js, :], in0=gate[GATE_F][:, js, :], in1=cx_t[:, js, :])
+                if g == GATE_G:
+                    nc.vector.tensor_mul(out=fresh[:, js, :], in0=gate[GATE_I][:, js, :], in1=gate[GATE_G][:, js, :])
+                    nc.vector.tensor_add(out=cx_new[:, js, :], in0=kept[:, js, :], in1=fresh[:, js, :])
+                    nc.scalar.activation(out=tanh_c[:, js, :], in_=cx_new[:, js, :], func=FUNC.Tanh)
+                if g == GATE_O:
+                    nc.vector.tensor_mul(out=hx_new[:, js, :], in0=gate[GATE_O][:, js, :], in1=tanh_c[:, js, :])
+                    nc.vector.tensor_copy(
+                        out=hx_grouped[:, :, js], in_=hx_new[:, js, :].rearrange("p j b -> p b j")
+                    )
 
         def store_batch_major(value_t, dram_out, label):
             bank = other_banks.tile([P, BLOCKS, P], F32, tag="other", name="bank_" + label)
@@ -133,64 +186,63 @@ def tile_actor_pa_s_kernel(
             )
             nc.sync.dma_start(out=dram_out, in_=rows[:])
 
-        gate = {}
-        for g in range(GATES):
-            w_codes = {}
-            w_scales = {}
-            for s in range(2):
-                w_words = w_raw[s, g][:].bitcast(F32)
-                grouped = regroup.tile([P, BLOCKS * P * PACK], BF16, align_bytes=64, tag="grouped")
-                grouped_words = grouped[:].bitcast(F32)
-                for half in range(2):
-                    bank = weight_banks.tile([P, SLOTS, P], F32, tag="weights")
-                    cols = slice(half * SLOTS * P, (half + 1) * SLOTS * P)
-                    transpose_four(nc, bank, w_words[:, cols], ident[:])
-                    copy = nc.vector.tensor_copy if (s == 1 and half == 1) else nc.scalar.copy
-                    copy_pairs_side_by_side(copy, grouped_words[:, cols], bank)
-                w_codes[s] = mx.tile([P, BLOCKS * P], U32, align_bytes=64, name="w_codes_%d_%d" % (s, g))
-                w_scales[s] = mx.tile([P, BLOCKS * P], U8, align_bytes=64, name="w_scales_%d_%d" % (s, g))
+        transpose_weights(0, GATE_I)
+        empty_banks(0)
+
+        x_bank = other_banks.tile([P, SLOTS, P], F32, tag="other")
+        transpose_four(nc, x_bank, x_raw[:].bitcast(F32), ident[:])
+        x_grouped = work.tile([P, 2 * BATCH * PACK], BF16, align_bytes=64)
+        copy_pairs_side_by_side(nc.vector.tensor_copy, x_grouped, x_bank)
+        x_codes = mx.tile([P, 2 * BATCH], U32, align_bytes=64)
+        x_scales = mx.tile([P, 2 * BATCH], U8, align_bytes=64)
+        nc.vector.quantize_mx(out=x_codes[:].bitcast(FP8X4), scales=x_scales[:], in_=x_grouped[:])
+
+        quantise_weights(0, GATE_I)
+        transpose_weights(1, GATE_I)
+        empty_banks(1)
+        quantise_weights(1, GATE_I)
+
+        cx_t = other_banks.tile([P, BLOCKS, BATCH], BF16, tag="other")
+        cx_blocks = cx_raw[:].rearrange("b (p j) -> b j p", j=BLOCKS)
+        for j in range(BLOCKS):
+            nc.tensor.transpose(cx_t[:, j, :], cx_blocks[:, j, :], ident_bf16[:])
+        bias = work.tile([P, GATES * BLOCKS], F32)
+        nc.vector.tensor_add(
+            out=bias[:], in0=b_raw[:, 0 : GATES * BLOCKS], in1=b_raw[:, GATES * BLOCKS :]
+        )
+
+        for g in range(1, GATES):
+            transpose_weights(0, g)
+            empty_banks(0)
+            quantise_weights(0, g)
+
+            if g == GATE_F:
+                fc3_bank = other_banks.tile([P, 2, P], F32, tag="other")
+                fc3_words = fc3_raw[:].bitcast(F32).rearrange("a (p u) -> a u p", u=2)
+                for u in range(2):
+                    nc.tensor.transpose(fc3_bank[:, u, :], fc3_words[:, u, :], ident[:])
+                fc3_grouped = work.tile([P, ACTIONS * PACK], BF16, align_bytes=64)
+                nc.vector.tensor_copy(
+                    out=fc3_grouped[:].bitcast(F32).rearrange("p (a u) -> p a u", u=2),
+                    in_=fc3_bank[:].rearrange("p u a -> p a u"),
+                )
+                fc3_codes = mx.tile([P, ACTIONS], U32, align_bytes=64)
+                fc3_scales = mx.tile([P, ACTIONS], U8, align_bytes=64)
                 nc.vector.quantize_mx(
-                    out=w_codes[s][:].bitcast(FP8X4), scales=w_scales[s][:], in_=grouped[:]
+                    out=fc3_codes[:].bitcast(FP8X4), scales=fc3_scales[:], in_=fc3_grouped[:]
                 )
 
-            gate_bank = gate_banks.tile([P, BLOCKS, BATCH], F32, tag="gate")
-            gate[g] = work.tile([P, BLOCKS, BATCH], F32, name="gate_%d" % g)
-            for j in range(BLOCKS):
-                for s in range(2):
-                    nc.tensor.matmul_mx(
-                        out=gate_bank[:, j, :],
-                        lhsT=w_codes[s][:, j * P : (j + 1) * P].bitcast(FP8X4),
-                        lhsT_scale=w_scales[s][:, j * P : (j + 1) * P],
-                        rhs=x_codes[:, s * BATCH : (s + 1) * BATCH].bitcast(FP8X4),
-                        rhs_scale=x_scales[:, s * BATCH : (s + 1) * BATCH],
-                        start=(s == 0),
-                        stop=(s == 1),
-                    )
-            for j in range(BLOCKS):
-                nc.scalar.activation(
-                    out=gate[g][:, j, :],
-                    in_=gate_bank[:, j, :],
-                    func=FUNC.Tanh if g == 2 else FUNC.Sigmoid,
-                    bias=bias[:, g * BLOCKS + j : g * BLOCKS + j + 1],
-                )
+            transpose_weights(1, g)
+            empty_banks(1)
+            multiply_and_activate(g - 1)
+            quantise_weights(1, g)
+            combine(g - 1)
 
-            if g == 1:
-                kept = work.tile([P, BLOCKS, BATCH], F32)
-                nc.vector.tensor_mul(out=kept[:], in0=gate[1][:], in1=cx_t[:])
-            if g == 2:
-                fresh = work.tile([P, BLOCKS, BATCH], F32)
-                nc.vector.tensor_mul(out=fresh[:], in0=gate[0][:], in1=gate[2][:])
-                cx_new = work.tile([P, BLOCKS, BATCH], F32)
-                nc.vector.tensor_add(out=cx_new[:], in0=kept[:], in1=fresh[:])
-                tanh_c = work.tile([P, BLOCKS, BATCH], F32)
-                nc.scalar.activation(out=tanh_c[:], in_=cx_new[:], func=FUNC.Tanh)
-                store_batch_major(cx_new, out_2, "cx")
+        multiply_and_activate(GATE_O)
+        store_batch_major(cx_new, out_2, "cx")
+        combine(GATE_O)
+        store_batch_major(hx_new, out_1, "hx")
 
-        hx_new = work.tile([P, BLOCKS, BATCH], F32)
-        nc.vector.tensor_mul(out=hx_new[:], in0=gate[3][:], in1=tanh_c[:])
-
-        hx_grouped = work.tile([P, BATCH, PACK], BF16, align_bytes=64)
-        nc.vector.tensor_copy(out=hx_grouped[:], in_=hx_new[:].rearrange("p j b -> p b j"))
         hx_codes = mx.tile([P, BATCH], U32, align_bytes=64)
         hx_scales = mx.tile([P, BATCH], U8, align_bytes=64)
         nc.vector.quantize_mx(
@@ -198,8 +250,6 @@ def tile_actor_pa_s_kernel(
             scales=hx_scales[:],
             in_=hx_grouped[:].rearrange("p b j -> p (b j)"),
         )
-        store_batch_major(hx_new, out_1, "hx")
-
         act_bank = other_banks.tile([P, ACTIONS], F32, tag="other")
         nc.tensor.matmul_mx(
             out=act_bank[:],

@@ -22,6 +22,8 @@ PACK = 4
 SLOTS = 4
 HALVES = 2
 HALF_BLOCKS = BLOCKS // HALVES
+WARM_PASSES = 32
+FILL_PASSES = 4
 
 FLOPS = 2 * BATCH * K * (2 * GATES * HIDDEN + ACTIONS)
 
@@ -87,6 +89,27 @@ def tile_actor_pa_s_kernel(
         for g in (GATE_G, GATE_O):
             for s in range(2):
                 load_weights(s, g)
+
+        zeros = consts.tile([P, P * PACK], BF16, align_bytes=64)
+        nc.vector.memset(zeros[:], 0.0)
+        zero_codes = consts.tile([P, P], U32, align_bytes=64)
+        zero_scales = consts.tile([P, P], U8, align_bytes=64)
+        nc.vector.quantize_mx(out=zero_codes[:].bitcast(FP8X4), scales=zero_scales[:], in_=zeros[:])
+
+        def idle_passes(count):
+            unread = gate_banks.tile([P, P], F32, tag="gate")
+            for i in range(count):
+                nc.tensor.matmul_mx(
+                    out=unread[:],
+                    lhsT=zero_codes[:].bitcast(FP8X4),
+                    lhsT_scale=zero_scales[:],
+                    rhs=zero_codes[:].bitcast(FP8X4),
+                    rhs_scale=zero_scales[:],
+                    start=True,
+                    stop=True,
+                )
+
+        idle_passes(WARM_PASSES)
 
         ident = consts.tile([P, P], F32)
         make_identity(nc, ident[:])
@@ -187,6 +210,7 @@ def tile_actor_pa_s_kernel(
             nc.sync.dma_start(out=dram_out, in_=rows[:])
 
         transpose_weights(0, GATE_I)
+        idle_passes(FILL_PASSES)
         empty_banks(0)
 
         x_bank = other_banks.tile([P, SLOTS, P], F32, tag="other")
@@ -199,6 +223,7 @@ def tile_actor_pa_s_kernel(
 
         quantise_weights(0, GATE_I)
         transpose_weights(1, GATE_I)
+        idle_passes(FILL_PASSES)
         empty_banks(1)
         quantise_weights(1, GATE_I)
 
@@ -213,6 +238,8 @@ def tile_actor_pa_s_kernel(
 
         for g in range(1, GATES):
             transpose_weights(0, g)
+            if g == GATE_F:
+                idle_passes(FILL_PASSES)
             empty_banks(0)
             quantise_weights(0, g)
 

@@ -22,8 +22,7 @@ PACK = 4
 SLOTS = 4
 HALVES = 2
 HALF_BLOCKS = BLOCKS // HALVES
-WARM_PASSES = 32
-FILL_PASSES = 4
+FC3_B_ROW = 2 * GATES
 
 FLOPS = 2 * BATCH * K * (2 * GATES * HIDDEN + ACTIONS)
 
@@ -70,46 +69,22 @@ def tile_actor_pa_s_kernel(
         nc.sync.dma_start(out=x_raw[:, 0:K], in_=h_fc2)
         nc.sync.dma_start(out=x_raw[:, K : 2 * K], in_=hx)
         load_weights(1, 0)
-        b_raw = raw.tile([P, 2 * GATES * BLOCKS], BF16)
-        for s, b in enumerate((b_ih, b_hh)):
-            nc.sync.dma_start(
-                out=b_raw[:, s * GATES * BLOCKS : (s + 1) * GATES * BLOCKS].rearrange(
-                    "p (g j) -> p g j", j=BLOCKS
-                ),
-                in_=b.rearrange("(g p j) -> p g j", g=GATES, j=BLOCKS),
-            )
+        b_rows = raw.tile([P, HIDDEN], BF16)
+        nc.vector.memset(b_rows[:], 0.0)
+        nc.sync.dma_start(out=b_rows[0:GATES, :], in_=b_ih.rearrange("(g h) -> g h", g=GATES))
+        nc.sync.dma_start(out=b_rows[GATES : 2 * GATES, :], in_=b_hh.rearrange("(g h) -> g h", g=GATES))
+        nc.sync.dma_start(
+            out=b_rows[FC3_B_ROW : FC3_B_ROW + 1, 0:ACTIONS], in_=fc3_b.rearrange("(o a) -> o a", o=1)
+        )
         cx_raw = raw.tile([P, HIDDEN], BF16)
         nc.sync.dma_start(out=cx_raw[:], in_=cx)
         load_weights(0, 1)
         fc3_raw = raw.tile([P, K], BF16)
         nc.sync.dma_start(out=fc3_raw[:], in_=fc3_w)
-        fc3_b_rows = raw.tile([P, ACTIONS], BF16)
-        nc.sync.dma_start(out=fc3_b_rows[:], in_=fc3_b.partition_broadcast(P))
         load_weights(1, 1)
         for g in (GATE_G, GATE_O):
             for s in range(2):
                 load_weights(s, g)
-
-        zeros = consts.tile([P, P * PACK], BF16, align_bytes=64)
-        nc.vector.memset(zeros[:], 0.0)
-        zero_codes = consts.tile([P, P], U32, align_bytes=64)
-        zero_scales = consts.tile([P, P], U8, align_bytes=64)
-        nc.vector.quantize_mx(out=zero_codes[:].bitcast(FP8X4), scales=zero_scales[:], in_=zeros[:])
-
-        def idle_passes(count):
-            unread = gate_banks.tile([P, P], F32, tag="gate")
-            for i in range(count):
-                nc.tensor.matmul_mx(
-                    out=unread[:],
-                    lhsT=zero_codes[:].bitcast(FP8X4),
-                    lhsT_scale=zero_scales[:],
-                    rhs=zero_codes[:].bitcast(FP8X4),
-                    rhs_scale=zero_scales[:],
-                    start=True,
-                    stop=True,
-                )
-
-        idle_passes(WARM_PASSES)
 
         ident = consts.tile([P, P], F32)
         make_identity(nc, ident[:])
@@ -173,7 +148,7 @@ def tile_actor_pa_s_kernel(
                         out=gate[g][:, j, :],
                         in_=gate_bank[:, i, :],
                         func=FUNC.Tanh if g == GATE_G else FUNC.Sigmoid,
-                        bias=bias[:, g * BLOCKS + j : g * BLOCKS + j + 1],
+                        bias=bias[:, j, g : g + 1],
                     )
 
         kept = work.tile([P, BLOCKS, BATCH], F32)
@@ -210,7 +185,6 @@ def tile_actor_pa_s_kernel(
             nc.sync.dma_start(out=dram_out, in_=rows[:])
 
         transpose_weights(0, GATE_I)
-        idle_passes(FILL_PASSES)
         empty_banks(0)
 
         x_bank = other_banks.tile([P, SLOTS, P], F32, tag="other")
@@ -223,23 +197,35 @@ def tile_actor_pa_s_kernel(
 
         quantise_weights(0, GATE_I)
         transpose_weights(1, GATE_I)
-        idle_passes(FILL_PASSES)
         empty_banks(1)
         quantise_weights(1, GATE_I)
+
+        b_t = other_banks.tile([P, BLOCKS, P], BF16, tag="other")
+        b_blocks = b_rows[:].rearrange("r (p j) -> r j p", j=BLOCKS)
+        for j in range(BLOCKS):
+            nc.tensor.transpose(b_t[:, j, :], b_blocks[:, j, :], ident_bf16[:])
+        b_cols = work.tile([P, BLOCKS, 2 * GATES], F32)
+        nc.vector.tensor_copy(out=b_cols[:], in_=b_t[:, :, 0 : 2 * GATES])
+        bias = work.tile([P, BLOCKS, GATES], F32)
+        nc.vector.tensor_add(out=bias[:], in0=b_cols[:, :, 0:GATES], in1=b_cols[:, :, GATES : 2 * GATES])
+        fc3_b_bank = other_banks.tile([P, ACTIONS], F32, tag="other")
+        nc.tensor.matmul(
+            out=fc3_b_bank[:],
+            lhsT=ident_bf16[:, FC3_B_ROW : FC3_B_ROW + 1].to_broadcast([P, P]),
+            rhs=b_rows[:, 0:ACTIONS],
+            start=True,
+            stop=True,
+        )
+        fc3_b_rows = work.tile([P, ACTIONS], F32)
+        nc.vector.tensor_copy(out=fc3_b_rows[:], in_=fc3_b_bank[:])
 
         cx_t = other_banks.tile([P, BLOCKS, BATCH], BF16, tag="other")
         cx_blocks = cx_raw[:].rearrange("b (p j) -> b j p", j=BLOCKS)
         for j in range(BLOCKS):
             nc.tensor.transpose(cx_t[:, j, :], cx_blocks[:, j, :], ident_bf16[:])
-        bias = work.tile([P, GATES * BLOCKS], F32)
-        nc.vector.tensor_add(
-            out=bias[:], in0=b_raw[:, 0 : GATES * BLOCKS], in1=b_raw[:, GATES * BLOCKS :]
-        )
 
         for g in range(1, GATES):
             transpose_weights(0, g)
-            if g == GATE_F:
-                idle_passes(FILL_PASSES)
             empty_banks(0)
             quantise_weights(0, g)
 

@@ -14,15 +14,19 @@ P = 128
 BATCH = 128
 K = 512
 HIDDEN = 512
+ACTIONS = 128
+PACK = 4
 BLOCKS = HIDDEN // P
 GATE_I, GATE_F, GATE_G, GATE_O = 0, 1, 2, 3
 GATES = 4
-ACTIONS = 128
-PACK = 4
-SLOTS = 4
+CHUNKS = 2 * GATES
 HALVES = 2
 HALF_BLOCKS = BLOCKS // HALVES
+HALF_GATES = GATES * HALVES
+SLOTS = 4
 FC3_B_ROW = 2 * GATES
+MATMUL_LAG = 2
+COMBINE_LAG = 3
 
 FLOPS = 2 * BATCH * K * (2 * GATES * HIDDEN + ACTIONS)
 
@@ -54,37 +58,39 @@ def tile_actor_pa_s_kernel(
         gate_banks = ctx.enter_context(tc.psum_pool(name="gate_banks", bufs=2))
         other_banks = ctx.enter_context(tc.psum_pool(name="other_banks", bufs=2))
 
-        w_raw = {}
+        x_raw = raw.tile([P, 2 * K], BF16)
+        b_rows = raw.tile([P, HIDDEN], BF16)
+        cx_raw = raw.tile([P, HIDDEN], BF16)
+        fc3_raw = raw.tile([P, K], BF16)
+        w_raw = [raw.tile([P, BLOCKS * K], BF16, name="w_raw_%d" % c) for c in range(CHUNKS)]
 
-        def load_weights(s, g):
-            w = (w_ih, w_hh)[s]
-            w_raw[s, g] = raw.tile([P, BLOCKS * K], BF16, name="w_raw_%d_%d" % (s, g))
+        def load_x():
+            nc.sync.dma_start(out=x_raw[:, 0:K], in_=h_fc2)
+            nc.sync.dma_start(out=x_raw[:, K : 2 * K], in_=hx)
+
+        def load_biases():
+            nc.vector.memset(b_rows[:], 0.0)
+            nc.sync.dma_start(out=b_rows[0:GATES, :], in_=b_ih.rearrange("(g h) -> g h", g=GATES))
+            nc.sync.dma_start(out=b_rows[GATES : 2 * GATES, :], in_=b_hh.rearrange("(g h) -> g h", g=GATES))
             nc.sync.dma_start(
-                out=w_raw[s, g][:],
-                in_=w[g * HIDDEN : (g + 1) * HIDDEN, :].rearrange("(p j) k -> p (j k)", j=BLOCKS),
+                out=b_rows[FC3_B_ROW : FC3_B_ROW + 1, 0:ACTIONS], in_=fc3_b.rearrange("(o a) -> o a", o=1)
             )
 
-        load_weights(0, 0)
-        x_raw = raw.tile([P, 2 * K], BF16)
-        nc.sync.dma_start(out=x_raw[:, 0:K], in_=h_fc2)
-        nc.sync.dma_start(out=x_raw[:, K : 2 * K], in_=hx)
-        load_weights(1, 0)
-        b_rows = raw.tile([P, HIDDEN], BF16)
-        nc.vector.memset(b_rows[:], 0.0)
-        nc.sync.dma_start(out=b_rows[0:GATES, :], in_=b_ih.rearrange("(g h) -> g h", g=GATES))
-        nc.sync.dma_start(out=b_rows[GATES : 2 * GATES, :], in_=b_hh.rearrange("(g h) -> g h", g=GATES))
-        nc.sync.dma_start(
-            out=b_rows[FC3_B_ROW : FC3_B_ROW + 1, 0:ACTIONS], in_=fc3_b.rearrange("(o a) -> o a", o=1)
-        )
-        cx_raw = raw.tile([P, HIDDEN], BF16)
-        nc.sync.dma_start(out=cx_raw[:], in_=cx)
-        load_weights(0, 1)
-        fc3_raw = raw.tile([P, K], BF16)
-        nc.sync.dma_start(out=fc3_raw[:], in_=fc3_w)
-        load_weights(1, 1)
-        for g in (GATE_G, GATE_O):
-            for s in range(2):
-                load_weights(s, g)
+        def load_cx():
+            nc.sync.dma_start(out=cx_raw[:], in_=cx)
+
+        def load_fc3_w():
+            nc.sync.dma_start(out=fc3_raw[:], in_=fc3_w)
+
+        small_loads = (load_x, load_biases, load_cx, load_fc3_w)
+        for c in range(CHUNKS):
+            g, s = divmod(c, 2)
+            nc.sync.dma_start(
+                out=w_raw[c][:],
+                in_=(w_ih, w_hh)[s][g * HIDDEN : (g + 1) * HIDDEN, :].rearrange("(p j) k -> p (j k)", j=BLOCKS),
+            )
+            if c < len(small_loads):
+                small_loads[c]()
 
         ident = consts.tile([P, P], F32)
         make_identity(nc, ident[:])
@@ -94,62 +100,110 @@ def tile_actor_pa_s_kernel(
         nc.vector.memset(warm[:], 0.0)
         nc.scalar.activation(out=warm[:], in_=warm[:], func=FUNC.Sigmoid)
 
-        banks = {}
-        grouped = {}
-        w_codes = {}
-        w_scales = {}
+        x_codes = mx.tile([P, 2 * BATCH], U32, align_bytes=64)
+        x_scales = mx.tile([P, 2 * BATCH], U8, align_bytes=64)
 
-        def transpose_weights(s, g):
-            w_words = w_raw[s, g][:].bitcast(F32)
+        def prepare_x():
+            x_bank = other_banks.tile([P, SLOTS, P], F32, tag="other")
+            transpose_four(nc, x_bank, x_raw[:].bitcast(F32), ident[:])
+            x_grouped = work.tile([P, 2 * BATCH * PACK], BF16, align_bytes=64)
+            copy_pairs_side_by_side(nc.vector.tensor_copy, x_grouped, x_bank)
+            nc.vector.quantize_mx(out=x_codes[:].bitcast(FP8X4), scales=x_scales[:], in_=x_grouped[:])
+
+        bias = work.tile([P, BLOCKS, GATES], F32)
+        fc3_b_rows = work.tile([P, ACTIONS], F32)
+
+        def prepare_biases():
+            b_t = other_banks.tile([P, BLOCKS, P], BF16, tag="other")
+            b_blocks = b_rows[:].rearrange("r (p j) -> r j p", j=BLOCKS)
+            for j in range(BLOCKS):
+                nc.tensor.transpose(b_t[:, j, :], b_blocks[:, j, :], ident_bf16[:])
+            b_cols = work.tile([P, BLOCKS, 2 * GATES], F32)
+            nc.vector.tensor_copy(out=b_cols[:], in_=b_t[:, :, 0 : 2 * GATES])
+            nc.vector.tensor_add(out=bias[:], in0=b_cols[:, :, 0:GATES], in1=b_cols[:, :, GATES : 2 * GATES])
+            fc3_b_bank = other_banks.tile([P, ACTIONS], F32, tag="other")
+            nc.tensor.matmul(
+                out=fc3_b_bank[:],
+                lhsT=ident_bf16[:, FC3_B_ROW : FC3_B_ROW + 1].to_broadcast([P, P]),
+                rhs=b_rows[:, 0:ACTIONS],
+                start=True,
+                stop=True,
+            )
+            nc.vector.tensor_copy(out=fc3_b_rows[:], in_=fc3_b_bank[:])
+
+        in_psum = {}
+
+        def prepare_cx():
+            in_psum["cx_t"] = other_banks.tile([P, BLOCKS, BATCH], BF16, tag="other", name="cx_t")
+            cx_blocks = cx_raw[:].rearrange("b (p j) -> b j p", j=BLOCKS)
+            for j in range(BLOCKS):
+                nc.tensor.transpose(in_psum["cx_t"][:, j, :], cx_blocks[:, j, :], ident_bf16[:])
+
+        fc3_codes = mx.tile([P, ACTIONS], U32, align_bytes=64)
+        fc3_scales = mx.tile([P, ACTIONS], U8, align_bytes=64)
+
+        def prepare_fc3_w():
+            fc3_bank = other_banks.tile([P, 2, P], F32, tag="other")
+            fc3_words = fc3_raw[:].bitcast(F32).rearrange("a (p u) -> a u p", u=2)
+            for u in range(2):
+                nc.tensor.transpose(fc3_bank[:, u, :], fc3_words[:, u, :], ident[:])
+            fc3_grouped = work.tile([P, ACTIONS * PACK], BF16, align_bytes=64)
+            nc.vector.tensor_copy(
+                out=fc3_grouped[:].bitcast(F32).rearrange("p (a u) -> p a u", u=2),
+                in_=fc3_bank[:].rearrange("p u a -> p a u"),
+            )
+            nc.vector.quantize_mx(out=fc3_codes[:].bitcast(FP8X4), scales=fc3_scales[:], in_=fc3_grouped[:])
+
+        side_work = (prepare_x, prepare_biases, prepare_cx, prepare_fc3_w)
+
+        w_codes = [mx.tile([P, BLOCKS * P], U32, align_bytes=64, name="w_codes_%d" % c) for c in range(CHUNKS)]
+        w_scales = [mx.tile([P, BLOCKS * P], U8, align_bytes=64, name="w_scales_%d" % c) for c in range(CHUNKS)]
+        grouped = {}
+
+        def transpose_and_empty(c):
+            w_words = w_raw[c][:].bitcast(F32)
+            banks = {}
             for half in range(HALVES):
                 banks[half] = weight_banks.tile([P, SLOTS, P], F32, tag="weights", name="bank_%d" % half)
                 transpose_four(nc, banks[half], w_words[:, half * SLOTS * P : (half + 1) * SLOTS * P], ident[:])
-
-        def empty_banks(s):
             for half in range(HALVES):
                 grouped[half] = regroup.tile(
                     [P, HALF_BLOCKS * P * PACK], BF16, align_bytes=64, tag="grouped", name="grouped_%d" % half
                 )
-                copy = nc.vector.tensor_copy if (s == 0 and half == 1) else nc.scalar.copy
+                copy = nc.vector.tensor_copy if (c % 2 == 0 and half == 1) else nc.scalar.copy
                 copy_pairs_side_by_side(copy, grouped[half], banks[half])
 
-        def quantise_weights(s, g):
-            w_codes[s, g] = mx.tile([P, BLOCKS * P], U32, align_bytes=64, name="w_codes_%d_%d" % (s, g))
-            w_scales[s, g] = mx.tile([P, BLOCKS * P], U8, align_bytes=64, name="w_scales_%d_%d" % (s, g))
+        def quantise(c):
             for half in range(HALVES):
                 cols = slice(half * HALF_BLOCKS * P, (half + 1) * HALF_BLOCKS * P)
                 nc.vector.quantize_mx(
-                    out=w_codes[s, g][:, cols].bitcast(FP8X4),
-                    scales=w_scales[s, g][:, cols],
-                    in_=grouped[half][:],
+                    out=w_codes[c][:, cols].bitcast(FP8X4), scales=w_scales[c][:, cols], in_=grouped[half][:]
                 )
 
-        gate = {}
+        gate = [work.tile([P, BLOCKS, BATCH], F32, name="gate_%d" % g) for g in range(GATES)]
 
-        def multiply_and_activate(g):
-            gate[g] = work.tile([P, BLOCKS, BATCH], F32, name="gate_%d" % g)
-            for half in range(HALVES):
-                gate_bank = gate_banks.tile([P, HALF_BLOCKS, BATCH], F32, tag="gate")
-                for i in range(HALF_BLOCKS):
-                    j = half * HALF_BLOCKS + i
-                    for s in range(2):
-                        nc.tensor.matmul_mx(
-                            out=gate_bank[:, i, :],
-                            lhsT=w_codes[s, g][:, j * P : (j + 1) * P].bitcast(FP8X4),
-                            lhsT_scale=w_scales[s, g][:, j * P : (j + 1) * P],
-                            rhs=x_codes[:, s * BATCH : (s + 1) * BATCH].bitcast(FP8X4),
-                            rhs_scale=x_scales[:, s * BATCH : (s + 1) * BATCH],
-                            start=(s == 0),
-                            stop=(s == 1),
-                        )
-                for i in range(HALF_BLOCKS):
-                    j = half * HALF_BLOCKS + i
-                    nc.scalar.activation(
-                        out=gate[g][:, j, :],
-                        in_=gate_bank[:, i, :],
-                        func=FUNC.Tanh if g == GATE_G else FUNC.Sigmoid,
-                        bias=bias[:, j, g : g + 1],
+        def multiply_and_activate(g, half):
+            gate_bank = gate_banks.tile([P, HALF_BLOCKS, BATCH], F32, tag="gate")
+            for i in range(HALF_BLOCKS):
+                j = half * HALF_BLOCKS + i
+                for s in range(2):
+                    nc.tensor.matmul_mx(
+                        out=gate_bank[:, i, :],
+                        lhsT=w_codes[2 * g + s][:, j * P : (j + 1) * P].bitcast(FP8X4),
+                        lhsT_scale=w_scales[2 * g + s][:, j * P : (j + 1) * P],
+                        rhs=x_codes[:, s * BATCH : (s + 1) * BATCH].bitcast(FP8X4),
+                        rhs_scale=x_scales[:, s * BATCH : (s + 1) * BATCH],
+                        start=(s == 0),
+                        stop=(s == 1),
                     )
+            for i in range(HALF_BLOCKS):
+                j = half * HALF_BLOCKS + i
+                nc.scalar.activation(
+                    out=gate[g][:, j, :],
+                    in_=gate_bank[:, i, :],
+                    func=FUNC.Tanh if g == GATE_G else FUNC.Sigmoid,
+                    bias=bias[:, j, g : g + 1],
+                )
 
         kept = work.tile([P, BLOCKS, BATCH], F32)
         fresh = work.tile([P, BLOCKS, BATCH], F32)
@@ -158,22 +212,31 @@ def tile_actor_pa_s_kernel(
         hx_new = work.tile([P, BLOCKS, BATCH], F32)
         hx_grouped = work.tile([P, BATCH, PACK], BF16, align_bytes=64)
 
-        def combine(g):
-            for half in range(HALVES):
-                js = slice(half * HALF_BLOCKS, (half + 1) * HALF_BLOCKS)
-                if g == GATE_F:
-                    nc.vector.tensor_mul(out=kept[:, js, :], in0=gate[GATE_F][:, js, :], in1=cx_t[:, js, :])
-                if g == GATE_G:
-                    nc.vector.tensor_mul(out=fresh[:, js, :], in0=gate[GATE_I][:, js, :], in1=gate[GATE_G][:, js, :])
-                    nc.vector.tensor_add(out=cx_new[:, js, :], in0=kept[:, js, :], in1=fresh[:, js, :])
-                    nc.scalar.activation(out=tanh_c[:, js, :], in_=cx_new[:, js, :], func=FUNC.Tanh)
-                if g == GATE_O:
-                    nc.vector.tensor_mul(out=hx_new[:, js, :], in0=gate[GATE_O][:, js, :], in1=tanh_c[:, js, :])
-                    nc.vector.tensor_copy(
-                        out=hx_grouped[:, :, js], in_=hx_new[:, js, :].rearrange("p j b -> p b j")
-                    )
+        def combine(g, half):
+            js = slice(half * HALF_BLOCKS, (half + 1) * HALF_BLOCKS)
+            if g == GATE_F:
+                nc.vector.tensor_mul(out=kept[:, js, :], in0=gate[GATE_F][:, js, :], in1=in_psum["cx_t"][:, js, :])
+            if g == GATE_G:
+                nc.vector.tensor_mul(out=fresh[:, js, :], in0=gate[GATE_I][:, js, :], in1=gate[GATE_G][:, js, :])
+                nc.vector.tensor_add(out=cx_new[:, js, :], in0=kept[:, js, :], in1=fresh[:, js, :])
+                nc.scalar.activation(out=tanh_c[:, js, :], in_=cx_new[:, js, :], func=FUNC.Tanh)
+            if g == GATE_O:
+                nc.vector.tensor_mul(out=hx_new[:, js, :], in0=gate[GATE_O][:, js, :], in1=tanh_c[:, js, :])
+                nc.vector.tensor_copy(out=hx_grouped[:, :, js], in_=hx_new[:, js, :].rearrange("p j b -> p b j"))
 
-        def store_batch_major(value_t, dram_out, label):
+        for step in range(CHUNKS + COMBINE_LAG):
+            if step < CHUNKS:
+                transpose_and_empty(step)
+            if 0 <= step - MATMUL_LAG < HALF_GATES:
+                multiply_and_activate(*divmod(step - MATMUL_LAG, HALVES))
+            if step < CHUNKS:
+                quantise(step)
+            if 0 <= step - COMBINE_LAG < HALF_GATES:
+                combine(*divmod(step - COMBINE_LAG, HALVES))
+            if step < len(side_work):
+                side_work[step]()
+
+        for value_t, dram_out, label in ((cx_new, out_2, "cx"), (hx_new, out_1, "hx")):
             bank = other_banks.tile([P, BLOCKS, P], F32, tag="other", name="bank_" + label)
             for j in range(BLOCKS):
                 nc.tensor.transpose(bank[:, j, :], value_t[:, j, :], ident[:])
@@ -183,78 +246,6 @@ def tile_actor_pa_s_kernel(
                 in_=bank[:].rearrange("b j p -> b p j"),
             )
             nc.sync.dma_start(out=dram_out, in_=rows[:])
-
-        transpose_weights(0, GATE_I)
-        empty_banks(0)
-
-        x_bank = other_banks.tile([P, SLOTS, P], F32, tag="other")
-        transpose_four(nc, x_bank, x_raw[:].bitcast(F32), ident[:])
-        x_grouped = work.tile([P, 2 * BATCH * PACK], BF16, align_bytes=64)
-        copy_pairs_side_by_side(nc.vector.tensor_copy, x_grouped, x_bank)
-        x_codes = mx.tile([P, 2 * BATCH], U32, align_bytes=64)
-        x_scales = mx.tile([P, 2 * BATCH], U8, align_bytes=64)
-        nc.vector.quantize_mx(out=x_codes[:].bitcast(FP8X4), scales=x_scales[:], in_=x_grouped[:])
-
-        quantise_weights(0, GATE_I)
-        transpose_weights(1, GATE_I)
-        empty_banks(1)
-        quantise_weights(1, GATE_I)
-
-        b_t = other_banks.tile([P, BLOCKS, P], BF16, tag="other")
-        b_blocks = b_rows[:].rearrange("r (p j) -> r j p", j=BLOCKS)
-        for j in range(BLOCKS):
-            nc.tensor.transpose(b_t[:, j, :], b_blocks[:, j, :], ident_bf16[:])
-        b_cols = work.tile([P, BLOCKS, 2 * GATES], F32)
-        nc.vector.tensor_copy(out=b_cols[:], in_=b_t[:, :, 0 : 2 * GATES])
-        bias = work.tile([P, BLOCKS, GATES], F32)
-        nc.vector.tensor_add(out=bias[:], in0=b_cols[:, :, 0:GATES], in1=b_cols[:, :, GATES : 2 * GATES])
-        fc3_b_bank = other_banks.tile([P, ACTIONS], F32, tag="other")
-        nc.tensor.matmul(
-            out=fc3_b_bank[:],
-            lhsT=ident_bf16[:, FC3_B_ROW : FC3_B_ROW + 1].to_broadcast([P, P]),
-            rhs=b_rows[:, 0:ACTIONS],
-            start=True,
-            stop=True,
-        )
-        fc3_b_rows = work.tile([P, ACTIONS], F32)
-        nc.vector.tensor_copy(out=fc3_b_rows[:], in_=fc3_b_bank[:])
-
-        cx_t = other_banks.tile([P, BLOCKS, BATCH], BF16, tag="other")
-        cx_blocks = cx_raw[:].rearrange("b (p j) -> b j p", j=BLOCKS)
-        for j in range(BLOCKS):
-            nc.tensor.transpose(cx_t[:, j, :], cx_blocks[:, j, :], ident_bf16[:])
-
-        for g in range(1, GATES):
-            transpose_weights(0, g)
-            empty_banks(0)
-            quantise_weights(0, g)
-
-            if g == GATE_F:
-                fc3_bank = other_banks.tile([P, 2, P], F32, tag="other")
-                fc3_words = fc3_raw[:].bitcast(F32).rearrange("a (p u) -> a u p", u=2)
-                for u in range(2):
-                    nc.tensor.transpose(fc3_bank[:, u, :], fc3_words[:, u, :], ident[:])
-                fc3_grouped = work.tile([P, ACTIONS * PACK], BF16, align_bytes=64)
-                nc.vector.tensor_copy(
-                    out=fc3_grouped[:].bitcast(F32).rearrange("p (a u) -> p a u", u=2),
-                    in_=fc3_bank[:].rearrange("p u a -> p a u"),
-                )
-                fc3_codes = mx.tile([P, ACTIONS], U32, align_bytes=64)
-                fc3_scales = mx.tile([P, ACTIONS], U8, align_bytes=64)
-                nc.vector.quantize_mx(
-                    out=fc3_codes[:].bitcast(FP8X4), scales=fc3_scales[:], in_=fc3_grouped[:]
-                )
-
-            transpose_weights(1, g)
-            empty_banks(1)
-            multiply_and_activate(g - 1)
-            quantise_weights(1, g)
-            combine(g - 1)
-
-        multiply_and_activate(GATE_O)
-        store_batch_major(cx_new, out_2, "cx")
-        combine(GATE_O)
-        store_batch_major(hx_new, out_1, "hx")
 
         hx_codes = mx.tile([P, BATCH], U32, align_bytes=64)
         hx_scales = mx.tile([P, BATCH], U8, align_bytes=64)

@@ -48,7 +48,8 @@ def tile_actor_pa_s_kernel(
 ):
     nc = tc.nc
     with ExitStack() as ctx:
-        ctx.enter_context(tc.manual_schedule())
+        pinned = {mybir.EngineType.PE, mybir.EngineType.SP, mybir.EngineType.Pool}
+        ctx.enter_context(tc.manual_schedule(engines=pinned))
         consts = ctx.enter_context(tc.tile_pool(name="consts", bufs=1))
         raw = ctx.enter_context(tc.tile_pool(name="raw", bufs=1))
         regroup = ctx.enter_context(tc.tile_pool(name="regroup", bufs=4))
@@ -85,10 +86,12 @@ def tile_actor_pa_s_kernel(
         small_loads = (load_x, load_biases, load_cx, load_fc3_w)
         for c in range(CHUNKS):
             g, s = divmod(c, 2)
-            nc.sync.dma_start(
-                out=w_raw[c][:],
-                in_=(w_ih, w_hh)[s][g * HIDDEN : (g + 1) * HIDDEN, :].rearrange("(p j) k -> p (j k)", j=BLOCKS),
-            )
+            rows = (w_ih, w_hh)[s][g * HIDDEN : (g + 1) * HIDDEN, :].rearrange("(p j) k -> p (j k)", j=BLOCKS)
+            parts = HALVES if c == 0 else 1
+            width = BLOCKS * K // parts
+            for i in range(parts):
+                cols = slice(i * width, (i + 1) * width)
+                nc.sync.dma_start(out=w_raw[c][:, cols], in_=rows[:, cols])
             if c < len(small_loads):
                 small_loads[c]()
 
@@ -221,8 +224,12 @@ def tile_actor_pa_s_kernel(
                 nc.vector.tensor_add(out=cx_new[:, js, :], in0=kept[:, js, :], in1=fresh[:, js, :])
                 nc.scalar.activation(out=tanh_c[:, js, :], in_=cx_new[:, js, :], func=FUNC.Tanh)
             if g == GATE_O:
+                nc.vector.tensor_mul(
+                    out=hx_grouped[:, :, js],
+                    in0=gate[GATE_O][:, js, :].rearrange("p j b -> p b j"),
+                    in1=tanh_c[:, js, :].rearrange("p j b -> p b j"),
+                )
                 nc.vector.tensor_mul(out=hx_new[:, js, :], in0=gate[GATE_O][:, js, :], in1=tanh_c[:, js, :])
-                nc.vector.tensor_copy(out=hx_grouped[:, :, js], in_=hx_new[:, js, :].rearrange("p j b -> p b j"))
 
         for step in range(CHUNKS + COMBINE_LAG):
             if step < CHUNKS:

@@ -212,7 +212,6 @@ def tile_actor_pa_s_kernel(
         fresh = work.tile([P, BLOCKS, BATCH], F32)
         cx_new = work.tile([P, BLOCKS, BATCH], F32)
         tanh_c = work.tile([P, BLOCKS, BATCH], F32)
-        hx_new = work.tile([P, BLOCKS, BATCH], F32)
         hx_grouped = work.tile([P, BATCH, PACK], BF16, align_bytes=64)
 
         def combine(g, half):
@@ -220,8 +219,9 @@ def tile_actor_pa_s_kernel(
             if g == GATE_F:
                 nc.vector.tensor_mul(out=kept[:, js, :], in0=gate[GATE_F][:, js, :], in1=in_psum["cx_t"][:, js, :])
             if g == GATE_G:
-                nc.vector.tensor_mul(out=fresh[:, js, :], in0=gate[GATE_I][:, js, :], in1=gate[GATE_G][:, js, :])
-                nc.vector.tensor_add(out=cx_new[:, js, :], in0=kept[:, js, :], in1=fresh[:, js, :])
+                engine = nc.gpsimd if half == 0 else nc.vector
+                engine.tensor_mul(out=fresh[:, js, :], in0=gate[GATE_I][:, js, :], in1=gate[GATE_G][:, js, :])
+                engine.tensor_add(out=cx_new[:, js, :], in0=kept[:, js, :], in1=fresh[:, js, :])
                 nc.scalar.activation(out=tanh_c[:, js, :], in_=cx_new[:, js, :], func=FUNC.Tanh)
             if g == GATE_O:
                 nc.vector.tensor_mul(
@@ -229,7 +229,6 @@ def tile_actor_pa_s_kernel(
                     in0=gate[GATE_O][:, js, :].rearrange("p j b -> p b j"),
                     in1=tanh_c[:, js, :].rearrange("p j b -> p b j"),
                 )
-                nc.vector.tensor_mul(out=hx_new[:, js, :], in0=gate[GATE_O][:, js, :], in1=tanh_c[:, js, :])
 
         for step in range(CHUNKS + COMBINE_LAG):
             if step < CHUNKS:
@@ -243,16 +242,21 @@ def tile_actor_pa_s_kernel(
             if step < len(side_work):
                 side_work[step]()
 
-        for value_t, dram_out, label in ((cx_new, out_2, "cx"), (hx_new, out_1, "hx")):
+        def transpose_out(value_t, label):
             bank = other_banks.tile([P, BLOCKS, P], F32, tag="other", name="bank_" + label)
             for j in range(BLOCKS):
                 nc.tensor.transpose(bank[:, j, :], value_t[:, j, :], ident[:])
-            rows = work.tile([P, HIDDEN], F32, name="rows_" + label)
-            nc.scalar.copy(
-                out=rows[:].rearrange("b (p j) -> b p j", j=BLOCKS),
-                in_=bank[:].rearrange("b j p -> b p j"),
-            )
-            nc.sync.dma_start(out=dram_out, in_=rows[:])
+            return bank[:].rearrange("b j p -> b p j")
+
+        def by_unit(rows):
+            return rows[:].rearrange("b (p j) -> b p j", j=BLOCKS)
+
+        cx_turned = transpose_out(cx_new, "cx")
+        tanh_rows = work.tile([P, HIDDEN], F32)
+        nc.scalar.activation(out=by_unit(tanh_rows), in_=cx_turned, func=FUNC.Tanh)
+        cx_rows = work.tile([P, HIDDEN], F32)
+        nc.scalar.copy(out=by_unit(cx_rows), in_=cx_turned)
+        nc.sync.dma_start(out=out_2, in_=cx_rows[:])
 
         hx_codes = mx.tile([P, BATCH], U32, align_bytes=64)
         hx_scales = mx.tile([P, BATCH], U8, align_bytes=64)
@@ -261,7 +265,11 @@ def tile_actor_pa_s_kernel(
             scales=hx_scales[:],
             in_=hx_grouped[:].rearrange("p b j -> p (b j)"),
         )
-        act_bank = other_banks.tile([P, ACTIONS], F32, tag="other")
+        o_turned = transpose_out(gate[GATE_O], "o")
+        hx_rows = work.tile([P, HIDDEN], F32)
+        nc.vector.tensor_mul(out=by_unit(hx_rows), in0=o_turned, in1=by_unit(tanh_rows))
+        nc.sync.dma_start(out=out_1, in_=hx_rows[:])
+        act_bank = gate_banks.tile([P, ACTIONS], F32, tag="gate")
         nc.tensor.matmul_mx(
             out=act_bank[:],
             lhsT=hx_codes[:].bitcast(FP8X4),

@@ -219,9 +219,8 @@ def tile_actor_pa_s_kernel(
             if g == GATE_F:
                 nc.vector.tensor_mul(out=kept[:, js, :], in0=gate[GATE_F][:, js, :], in1=in_psum["cx_t"][:, js, :])
             if g == GATE_G:
-                engine = nc.gpsimd if half == 0 else nc.vector
-                engine.tensor_mul(out=fresh[:, js, :], in0=gate[GATE_I][:, js, :], in1=gate[GATE_G][:, js, :])
-                engine.tensor_add(out=cx_new[:, js, :], in0=kept[:, js, :], in1=fresh[:, js, :])
+                nc.vector.tensor_mul(out=fresh[:, js, :], in0=gate[GATE_I][:, js, :], in1=gate[GATE_G][:, js, :])
+                nc.vector.tensor_add(out=cx_new[:, js, :], in0=kept[:, js, :], in1=fresh[:, js, :])
                 nc.scalar.activation(out=tanh_c[:, js, :], in_=cx_new[:, js, :], func=FUNC.Tanh)
             if g == GATE_O:
                 nc.vector.tensor_mul(

@@ -26,9 +26,17 @@ HALF_GATES = GATES * HALVES
 SLOTS = 4
 FC3_B_ROW = 2 * GATES
 MATMUL_LAG = 2
+VECTOR_STEPS = (0, 1, 4, 6)
+SPLIT_STEPS = (0, 1, 6, 7)
 COMBINE_LAG = 3
 
 FLOPS = 2 * BATCH * K * (2 * GATES * HIDDEN + ACTIONS)
+
+
+def step_halves(step):
+    if step < CHUNKS - 2:
+        return (step, 0), (step, 1)
+    return (CHUNKS - 2, step - (CHUNKS - 2)), (CHUNKS - 1, step - (CHUNKS - 2))
 
 
 def transpose_four(nc, bank, words, ident):
@@ -48,8 +56,7 @@ def tile_actor_pa_s_kernel(
 ):
     nc = tc.nc
     with ExitStack() as ctx:
-        pinned = {mybir.EngineType.PE, mybir.EngineType.SP, mybir.EngineType.Pool}
-        ctx.enter_context(tc.manual_schedule(engines=pinned))
+        ctx.enter_context(tc.manual_schedule())
         consts = ctx.enter_context(tc.tile_pool(name="consts", bufs=1))
         raw = ctx.enter_context(tc.tile_pool(name="raw", bufs=1))
         regroup = ctx.enter_context(tc.tile_pool(name="regroup", bufs=4))
@@ -83,17 +90,21 @@ def tile_actor_pa_s_kernel(
         def load_fc3_w():
             nc.sync.dma_start(out=fc3_raw[:], in_=fc3_w)
 
-        small_loads = (load_x, load_biases, load_cx, load_fc3_w)
-        for c in range(CHUNKS):
+        small_loads = {1: load_x, 2: load_biases, 5: load_cx, 7: load_fc3_w}
+        def load_weights(c, halves):
             g, s = divmod(c, 2)
             rows = (w_ih, w_hh)[s][g * HIDDEN : (g + 1) * HIDDEN, :].rearrange("(p j) k -> p (j k)", j=BLOCKS)
-            parts = HALVES if c == 0 else 1
-            width = BLOCKS * K // parts
-            for i in range(parts):
-                cols = slice(i * width, (i + 1) * width)
-                nc.sync.dma_start(out=w_raw[c][:, cols], in_=rows[:, cols])
-            if c < len(small_loads):
-                small_loads[c]()
+            cols = slice(halves[0] * HALF_BLOCKS * K, (halves[-1] + 1) * HALF_BLOCKS * K)
+            nc.sync.dma_start(out=w_raw[c][:, cols], in_=rows[:, cols])
+
+        for step in range(CHUNKS):
+            if step in SPLIT_STEPS:
+                for c, half in step_halves(step):
+                    load_weights(c, (half,))
+            else:
+                load_weights(step, (0, 1))
+            if step in small_loads:
+                small_loads[step]()
 
         ident = consts.tile([P, P], F32)
         make_identity(nc, ident[:])
@@ -106,37 +117,46 @@ def tile_actor_pa_s_kernel(
         x_codes = mx.tile([P, 2 * BATCH], U32, align_bytes=64)
         x_scales = mx.tile([P, 2 * BATCH], U8, align_bytes=64)
 
-        def prepare_x():
-            x_bank = other_banks.tile([P, SLOTS, P], F32, tag="other")
-            transpose_four(nc, x_bank, x_raw[:].bitcast(F32), ident[:])
-            x_grouped = work.tile([P, 2 * BATCH * PACK], BF16, align_bytes=64)
-            copy_pairs_side_by_side(nc.vector.tensor_copy, x_grouped, x_bank)
+        in_psum = {}
+        x_grouped = work.tile([P, 2 * BATCH * PACK], BF16, align_bytes=64)
+
+        def transpose_x():
+            in_psum["x"] = other_banks.tile([P, SLOTS, P], F32, tag="other", name="x_bank")
+            transpose_four(nc, in_psum["x"], x_raw[:].bitcast(F32), ident[:])
+
+        def empty_x():
+            copy_pairs_side_by_side(nc.scalar.copy, x_grouped, in_psum["x"])
+
+        def quantise_x():
             nc.vector.quantize_mx(out=x_codes[:].bitcast(FP8X4), scales=x_scales[:], in_=x_grouped[:])
 
         bias = work.tile([P, BLOCKS, GATES], F32)
         fc3_b_rows = work.tile([P, ACTIONS], F32)
 
-        def prepare_biases():
-            b_t = other_banks.tile([P, BLOCKS, P], BF16, tag="other")
+        def transpose_biases():
+            in_psum["b"] = other_banks.tile([P, BLOCKS, P], BF16, tag="other", name="b_t")
             b_blocks = b_rows[:].rearrange("r (p j) -> r j p", j=BLOCKS)
             for j in range(BLOCKS):
-                nc.tensor.transpose(b_t[:, j, :], b_blocks[:, j, :], ident_bf16[:])
-            b_cols = work.tile([P, BLOCKS, 2 * GATES], F32)
-            nc.vector.tensor_copy(out=b_cols[:], in_=b_t[:, :, 0 : 2 * GATES])
-            nc.vector.tensor_add(out=bias[:], in0=b_cols[:, :, 0:GATES], in1=b_cols[:, :, GATES : 2 * GATES])
-            fc3_b_bank = other_banks.tile([P, ACTIONS], F32, tag="other")
+                nc.tensor.transpose(in_psum["b"][:, j, :], b_blocks[:, j, :], ident_bf16[:])
+
+        def spread_fc3_b():
+            in_psum["fc3_b"] = other_banks.tile([P, ACTIONS], F32, tag="other", name="fc3_b_bank")
             nc.tensor.matmul(
-                out=fc3_b_bank[:],
+                out=in_psum["fc3_b"][:],
                 lhsT=ident_bf16[:, FC3_B_ROW : FC3_B_ROW + 1].to_broadcast([P, P]),
                 rhs=b_rows[:, 0:ACTIONS],
                 start=True,
                 stop=True,
             )
-            nc.vector.tensor_copy(out=fc3_b_rows[:], in_=fc3_b_bank[:])
 
-        in_psum = {}
+        b_cols = work.tile([P, BLOCKS, 2 * GATES], F32)
 
-        def prepare_cx():
+        def add_biases():
+            nc.vector.tensor_copy(out=b_cols[:], in_=in_psum["b"][:, :, 0 : 2 * GATES])
+            nc.vector.tensor_copy(out=fc3_b_rows[:], in_=in_psum["fc3_b"][:])
+            nc.vector.tensor_add(out=bias[:], in0=b_cols[:, :, 0:GATES], in1=b_cols[:, :, GATES : 2 * GATES])
+
+        def transpose_cx():
             in_psum["cx_t"] = other_banks.tile([P, BLOCKS, BATCH], BF16, tag="other", name="cx_t")
             cx_blocks = cx_raw[:].rearrange("b (p j) -> b j p", j=BLOCKS)
             for j in range(BLOCKS):
@@ -145,48 +165,53 @@ def tile_actor_pa_s_kernel(
         fc3_codes = mx.tile([P, ACTIONS], U32, align_bytes=64)
         fc3_scales = mx.tile([P, ACTIONS], U8, align_bytes=64)
 
-        def prepare_fc3_w():
-            fc3_bank = other_banks.tile([P, 2, P], F32, tag="other")
+        fc3_grouped = work.tile([P, ACTIONS * PACK], BF16, align_bytes=64)
+
+        def transpose_fc3_w():
+            in_psum["fc3"] = other_banks.tile([P, 2, P], F32, tag="other", name="fc3_bank")
             fc3_words = fc3_raw[:].bitcast(F32).rearrange("a (p u) -> a u p", u=2)
             for u in range(2):
-                nc.tensor.transpose(fc3_bank[:, u, :], fc3_words[:, u, :], ident[:])
-            fc3_grouped = work.tile([P, ACTIONS * PACK], BF16, align_bytes=64)
-            nc.vector.tensor_copy(
-                out=fc3_grouped[:].bitcast(F32).rearrange("p (a u) -> p a u", u=2),
-                in_=fc3_bank[:].rearrange("p u a -> p a u"),
-            )
-            nc.vector.quantize_mx(out=fc3_codes[:].bitcast(FP8X4), scales=fc3_scales[:], in_=fc3_grouped[:])
+                nc.tensor.transpose(in_psum["fc3"][:, u, :], fc3_words[:, u, :], ident[:])
 
-        side_work = (prepare_x, prepare_biases, prepare_cx, prepare_fc3_w)
+        def empty_fc3_w():
+            nc.scalar.copy(
+                out=fc3_grouped[:].bitcast(F32).rearrange("p (a u) -> p a u", u=2),
+                in_=in_psum["fc3"][:].rearrange("p u a -> p a u"),
+            )
+
+        def quantise_fc3_w():
+            nc.vector.quantize_mx(out=fc3_codes[:].bitcast(FP8X4), scales=fc3_scales[:], in_=fc3_grouped[:])
 
         w_codes = [mx.tile([P, BLOCKS * P], U32, align_bytes=64, name="w_codes_%d" % c) for c in range(CHUNKS)]
         w_scales = [mx.tile([P, BLOCKS * P], U8, align_bytes=64, name="w_scales_%d" % c) for c in range(CHUNKS)]
         grouped = {}
 
-        def transpose_and_empty(c):
-            w_words = w_raw[c][:].bitcast(F32)
-            banks = {}
-            for half in range(HALVES):
-                banks[half] = weight_banks.tile([P, SLOTS, P], F32, tag="weights", name="bank_%d" % half)
-                transpose_four(nc, banks[half], w_words[:, half * SLOTS * P : (half + 1) * SLOTS * P], ident[:])
-            for half in range(HALVES):
-                grouped[half] = regroup.tile(
-                    [P, HALF_BLOCKS * P * PACK], BF16, align_bytes=64, tag="grouped", name="grouped_%d" % half
-                )
-                copy = nc.vector.tensor_copy if (c % 2 == 0 and half == 1) else nc.scalar.copy
-                copy_pairs_side_by_side(copy, grouped[half], banks[half])
+        bank_of = {}
 
-        def quantise(c):
-            for half in range(HALVES):
-                cols = slice(half * HALF_BLOCKS * P, (half + 1) * HALF_BLOCKS * P)
-                nc.vector.quantize_mx(
-                    out=w_codes[c][:, cols].bitcast(FP8X4), scales=w_scales[c][:, cols], in_=grouped[half][:]
-                )
+        def transpose(c, half):
+            words = w_raw[c][:].bitcast(F32)
+            bank_of[c, half] = weight_banks.tile([P, SLOTS, P], F32, tag="weights", name="bank_%d_%d" % (c, half))
+            transpose_four(nc, bank_of[c, half], words[:, half * SLOTS * P : (half + 1) * SLOTS * P], ident[:])
+
+        def empty(copy, c, half):
+            grouped[c, half] = regroup.tile(
+                [P, HALF_BLOCKS * P * PACK], BF16, align_bytes=64, tag="grouped", name="grouped_%d_%d" % (c, half)
+            )
+            copy_pairs_side_by_side(copy, grouped[c, half], bank_of[c, half])
+
+        def quantise(c, half):
+            cols = slice(half * HALF_BLOCKS * P, (half + 1) * HALF_BLOCKS * P)
+            nc.vector.quantize_mx(
+                out=w_codes[c][:, cols].bitcast(FP8X4), scales=w_scales[c][:, cols], in_=grouped[c, half][:]
+            )
 
         gate = [work.tile([P, BLOCKS, BATCH], F32, name="gate_%d" % g) for g in range(GATES)]
 
-        def multiply_and_activate(g, half):
+        gate_bank_of = {}
+
+        def multiply(g, half):
             gate_bank = gate_banks.tile([P, HALF_BLOCKS, BATCH], F32, tag="gate")
+            gate_bank_of[g, half] = gate_bank
             for i in range(HALF_BLOCKS):
                 j = half * HALF_BLOCKS + i
                 for s in range(2):
@@ -199,11 +224,13 @@ def tile_actor_pa_s_kernel(
                         start=(s == 0),
                         stop=(s == 1),
                     )
+
+        def activate(g, half):
             for i in range(HALF_BLOCKS):
                 j = half * HALF_BLOCKS + i
                 nc.scalar.activation(
                     out=gate[g][:, j, :],
-                    in_=gate_bank[:, i, :],
+                    in_=gate_bank_of[g, half][:, i, :],
                     func=FUNC.Tanh if g == GATE_G else FUNC.Sigmoid,
                     bias=bias[:, j, g : g + 1],
                 )
@@ -214,71 +241,128 @@ def tile_actor_pa_s_kernel(
         tanh_c = work.tile([P, BLOCKS, BATCH], F32)
         hx_grouped = work.tile([P, BATCH, PACK], BF16, align_bytes=64)
 
-        def combine(g, half):
-            js = slice(half * HALF_BLOCKS, (half + 1) * HALF_BLOCKS)
-            if g == GATE_F:
-                nc.vector.tensor_mul(out=kept[:, js, :], in0=gate[GATE_F][:, js, :], in1=in_psum["cx_t"][:, js, :])
-            if g == GATE_G:
-                nc.vector.tensor_mul(out=fresh[:, js, :], in0=gate[GATE_I][:, js, :], in1=gate[GATE_G][:, js, :])
-                nc.vector.tensor_add(out=cx_new[:, js, :], in0=kept[:, js, :], in1=fresh[:, js, :])
-                nc.scalar.activation(out=tanh_c[:, js, :], in_=cx_new[:, js, :], func=FUNC.Tanh)
-            if g == GATE_O:
-                nc.vector.tensor_mul(
-                    out=hx_grouped[:, :, js],
-                    in0=gate[GATE_O][:, js, :].rearrange("p j b -> p b j"),
-                    in1=tanh_c[:, js, :].rearrange("p j b -> p b j"),
-                )
+        def of_half(value, half):
+            return value[:, half * HALF_BLOCKS : (half + 1) * HALF_BLOCKS, :]
 
-        for step in range(CHUNKS + COMBINE_LAG):
-            if step < CHUNKS:
-                transpose_and_empty(step)
-            if 0 <= step - MATMUL_LAG < HALF_GATES:
-                multiply_and_activate(*divmod(step - MATMUL_LAG, HALVES))
-            if step < CHUNKS:
-                quantise(step)
-            if 0 <= step - COMBINE_LAG < HALF_GATES:
-                combine(*divmod(step - COMBINE_LAG, HALVES))
-            if step < len(side_work):
-                side_work[step]()
+        def keep_cell(half):
+            nc.vector.tensor_mul(
+                out=of_half(kept, half), in0=of_half(gate[GATE_F], half), in1=of_half(in_psum["cx_t"], half)
+            )
 
-        def transpose_out(value_t, label):
-            bank = other_banks.tile([P, BLOCKS, P], F32, tag="other", name="bank_" + label)
+        def new_cell(half):
+            nc.vector.tensor_mul(
+                out=of_half(fresh, half), in0=of_half(gate[GATE_I], half), in1=of_half(gate[GATE_G], half)
+            )
+
+        def add_cell(half):
+            nc.vector.tensor_add(out=of_half(cx_new, half), in0=of_half(kept, half), in1=of_half(fresh, half))
+
+        def tanh_cell(half):
+            nc.scalar.activation(out=of_half(tanh_c, half), in_=of_half(cx_new, half), func=FUNC.Tanh)
+
+        def round_hx(half):
+            nc.vector.tensor_mul(
+                out=hx_grouped[:, :, half * HALF_BLOCKS : (half + 1) * HALF_BLOCKS],
+                in0=of_half(gate[GATE_O], half).rearrange("p j b -> p b j"),
+                in1=of_half(tanh_c, half).rearrange("p j b -> p b j"),
+            )
+
+        def turn(value_t, label):
+            bank = weight_banks.tile([P, SLOTS, P], F32, tag="weights", name="bank_" + label)
             for j in range(BLOCKS):
                 nc.tensor.transpose(bank[:, j, :], value_t[:, j, :], ident[:])
-            return bank[:].rearrange("b j p -> b p j")
+            in_psum[label] = bank[:].rearrange("b j p -> b p j")
 
         def by_unit(rows):
             return rows[:].rearrange("b (p j) -> b p j", j=BLOCKS)
 
-        cx_turned = transpose_out(cx_new, "cx")
-        tanh_rows = work.tile([P, HIDDEN], F32)
-        nc.scalar.activation(out=by_unit(tanh_rows), in_=cx_turned, func=FUNC.Tanh)
         cx_rows = work.tile([P, HIDDEN], F32)
-        nc.scalar.copy(out=by_unit(cx_rows), in_=cx_turned)
-        nc.sync.dma_start(out=out_2, in_=cx_rows[:])
-
+        tanh_rows = work.tile([P, HIDDEN], F32)
+        hx_rows = work.tile([P, HIDDEN], F32)
         hx_codes = mx.tile([P, BATCH], U32, align_bytes=64)
         hx_scales = mx.tile([P, BATCH], U8, align_bytes=64)
-        nc.vector.quantize_mx(
-            out=hx_codes[:].bitcast(FP8X4),
-            scales=hx_scales[:],
-            in_=hx_grouped[:].rearrange("p b j -> p (b j)"),
-        )
-        o_turned = transpose_out(gate[GATE_O], "o")
-        hx_rows = work.tile([P, HIDDEN], F32)
-        nc.vector.tensor_mul(out=by_unit(hx_rows), in0=o_turned, in1=by_unit(tanh_rows))
-        nc.sync.dma_start(out=out_1, in_=hx_rows[:])
-        act_bank = gate_banks.tile([P, ACTIONS], F32, tag="gate")
-        nc.tensor.matmul_mx(
-            out=act_bank[:],
-            lhsT=hx_codes[:].bitcast(FP8X4),
-            lhsT_scale=hx_scales[:],
-            rhs=fc3_codes[:].bitcast(FP8X4),
-            rhs_scale=fc3_scales[:],
-            start=True,
-            stop=True,
-        )
         act = work.tile([P, ACTIONS], F32)
-        nc.vector.tensor_add(out=act[:], in0=act_bank[:], in1=fc3_b_rows[:])
+
+        def quantise_hx():
+            nc.vector.quantize_mx(
+                out=hx_codes[:].bitcast(FP8X4),
+                scales=hx_scales[:],
+                in_=hx_grouped[:].rearrange("p b j -> p (b j)"),
+            )
+
+        def multiply_head():
+            in_psum["act"] = gate_banks.tile([P, ACTIONS], F32, tag="gate", name="act_bank")
+            nc.tensor.matmul_mx(
+                out=in_psum["act"][:],
+                lhsT=hx_codes[:].bitcast(FP8X4),
+                lhsT_scale=hx_scales[:],
+                rhs=fc3_codes[:].bitcast(FP8X4),
+                rhs_scale=fc3_scales[:],
+                start=True,
+                stop=True,
+            )
+
+        vec, sca = nc.vector.tensor_copy, nc.scalar.copy
+
+        for step in range(CHUNKS):
+            (c0, h0), (c1, h1) = step_halves(step)
+            transpose(c0, h0)
+            transpose(c1, h1)
+            if step == 1:
+                transpose_x()
+            if step == 2:
+                transpose_biases()
+                spread_fc3_b()
+            if step == 6:
+                transpose_cx()
+            if step >= 1:
+                for c, h in step_halves(step - 1):
+                    quantise(c, h)
+            if step == 1:
+                empty_x()
+            if step == 2:
+                quantise_x()
+            gate_done = (step - 3) // 2
+            if step >= 3 and (step - 3) % 2 == 0:
+                multiply(gate_done, 0)
+                multiply(gate_done, 1)
+            empty(sca, c0, h0)
+            empty(vec if step in VECTOR_STEPS else sca, c1, h1)
+            if step == 2:
+                add_biases()
+            if step >= 3 and (step - 3) % 2 == 0:
+                activate(gate_done, 0)
+                activate(gate_done, 1)
+
+        transpose_fc3_w()
+        quantise(CHUNKS - 2, 1)
+        keep_cell(0)
+        quantise(CHUNKS - 1, 1)
+        empty_fc3_w()
+        multiply(GATE_O, 0)
+        multiply(GATE_O, 1)
+        new_cell(0)
+        keep_cell(1)
+        new_cell(1)
+        activate(GATE_O, 0)
+        activate(GATE_O, 1)
+        add_cell(0)
+        add_cell(1)
+        tanh_cell(0)
+        tanh_cell(1)
+        quantise_fc3_w()
+        turn(cx_new, "cx")
+        turn(cx_new, "tanh")
+        turn(gate[GATE_O], "o")
+        nc.scalar.activation(out=by_unit(tanh_rows), in_=in_psum["tanh"], func=FUNC.Tanh)
+        round_hx(0)
+        round_hx(1)
+        nc.vector.tensor_copy(out=by_unit(cx_rows), in_=in_psum["cx"])
+        nc.sync.dma_start(out=out_2, in_=cx_rows[:])
+        quantise_hx()
+        multiply_head()
+        nc.vector.tensor_mul(out=by_unit(hx_rows), in0=in_psum["o"], in1=by_unit(tanh_rows))
+        nc.sync.dma_start(out=out_1, in_=hx_rows[:])
+        nc.vector.tensor_add(out=act[:], in0=in_psum["act"][:], in1=fc3_b_rows[:])
         nc.scalar.activation(out=act[:], in_=act[:], func=FUNC.Tanh)
         nc.sync.dma_start(out=out_0, in_=act[:])

@@ -27,7 +27,7 @@ SLOTS = 4
 FC3_B_ROW = 2 * GATES
 MATMUL_LAG = 2
 VECTOR_STEPS = (0, 1, 4, 6)
-SPLIT_STEPS = (0, 1, 6, 7)
+SPLIT_STEPS = (0, 6, 7)
 COMBINE_LAG = 3
 
 FLOPS = 2 * BATCH * K * (2 * GATES * HIDDEN + ACTIONS)
@@ -90,7 +90,7 @@ def tile_actor_pa_s_kernel(
         def load_fc3_w():
             nc.sync.dma_start(out=fc3_raw[:], in_=fc3_w)
 
-        small_loads = {1: load_x, 2: load_biases, 5: load_cx, 7: load_fc3_w}
+        small_loads = {0: load_x, 3: load_biases, 5: load_cx, 7: load_fc3_w}
         def load_weights(c, halves):
             g, s = divmod(c, 2)
             rows = (w_ih, w_hh)[s][g * HIDDEN : (g + 1) * HIDDEN, :].rearrange("(p j) k -> p (j k)", j=BLOCKS)
@@ -308,9 +308,9 @@ def tile_actor_pa_s_kernel(
             (c0, h0), (c1, h1) = step_halves(step)
             transpose(c0, h0)
             transpose(c1, h1)
-            if step == 1:
+            if step == 0:
                 transpose_x()
-            if step == 2:
+            if step == 3:
                 transpose_biases()
                 spread_fc3_b()
             if step == 6:
@@ -328,7 +328,7 @@ def tile_actor_pa_s_kernel(
                 multiply(gate_done, 1)
             empty(sca, c0, h0)
             empty(vec if step in VECTOR_STEPS else sca, c1, h1)
-            if step == 2:
+            if step == 3:
                 add_biases()
             if step >= 3 and (step - 3) % 2 == 0:
                 activate(gate_done, 0)

@@ -306,6 +306,8 @@ def tile_actor_pa_s_kernel(
 
         for step in range(CHUNKS):
             (c0, h0), (c1, h1) = step_halves(step)
+            if step == 6:
+                transpose_cx()
             transpose(c0, h0)
             transpose(c1, h1)
             if step == 0:
@@ -313,11 +315,13 @@ def tile_actor_pa_s_kernel(
             if step == 3:
                 transpose_biases()
                 spread_fc3_b()
-            if step == 6:
-                transpose_cx()
             if step >= 1:
                 for c, h in step_halves(step - 1):
                     quantise(c, h)
+            if step == 6:
+                keep_cell(0)
+            if step == 6:
+                keep_cell(1)
             if step == 1:
                 empty_x()
             if step == 2:
@@ -336,13 +340,11 @@ def tile_actor_pa_s_kernel(
 
         transpose_fc3_w()
         quantise(CHUNKS - 2, 1)
-        keep_cell(0)
         quantise(CHUNKS - 1, 1)
         empty_fc3_w()
         multiply(GATE_O, 0)
         multiply(GATE_O, 1)
         new_cell(0)
-        keep_cell(1)
         new_cell(1)
         activate(GATE_O, 0)
         activate(GATE_O, 1)
@@ -351,13 +353,14 @@ def tile_actor_pa_s_kernel(
         tanh_cell(0)
         tanh_cell(1)
         quantise_fc3_w()
-        turn(cx_new, "cx")
         turn(cx_new, "tanh")
+        turn(cx_new, "cx")
         turn(gate[GATE_O], "o")
         nc.scalar.activation(out=by_unit(tanh_rows), in_=in_psum["tanh"], func=FUNC.Tanh)
+        nc.scalar.copy(out=by_unit(cx_rows)[:, 64:, :], in_=in_psum["tanh"][:, 64:, :])
         round_hx(0)
         round_hx(1)
-        nc.vector.tensor_copy(out=by_unit(cx_rows), in_=in_psum["cx"])
+        nc.vector.tensor_copy(out=by_unit(cx_rows)[:, 0:64, :], in_=in_psum["cx"][:, 0:64, :])
         nc.sync.dma_start(out=out_2, in_=cx_rows[:])
         quantise_hx()
         multiply_head()

from contextlib import ExitStack

import concourse.mybir as mybir
from concourse.masks import make_identity

BF16 = mybir.dt.bfloat16
F32 = mybir.dt.float32
U32 = mybir.dt.uint32
U8 = mybir.dt.uint8
FP8X4 = mybir.dt.float8_e4m3fn_x4
FUNC = mybir.ActivationFunctionType

P = 128
BATCH = 128
K = 512
HIDDEN = 512
ACTIONS = 128
PACK = 4
BLOCKS = HIDDEN // P
GATE_I, GATE_F, GATE_G, GATE_O = 0, 1, 2, 3
GATES = 4
CHUNKS = 2 * GATES
HALVES = 2
HALF_BLOCKS = BLOCKS // HALVES
HALF_GATES = GATES * HALVES
SLOTS = 4
FC3_B_ROW = 2 * GATES
MATMUL_LAG = 2
VECTOR_STEPS = (0, 1, 4, 6)
SPLIT_STEPS = (0, 6, 7)
COMBINE_LAG = 3

FLOPS = 2 * BATCH * K * (2 * GATES * HIDDEN + ACTIONS)


def step_halves(step):
    if step < CHUNKS - 2:
        return (step, 0), (step, 1)
    return (CHUNKS - 2, step - (CHUNKS - 2)), (CHUNKS - 1, step - (CHUNKS - 2))


def transpose_four(nc, bank, words, ident):
    for t in range(SLOTS):
        nc.tensor.transpose(bank[:, t, :], words[:, t * P : (t + 1) * P], ident)


def copy_pairs_side_by_side(copy, grouped, bank):
    copy(
        out=grouped[:].bitcast(F32).rearrange("q (o c u) -> q o c u", o=2, u=2),
        in_=bank[:].rearrange("q (o u) c -> q o c u", u=2),
    )


def tile_actor_pa_s_kernel(
    tc, h_fc2, hx, cx, w_ih, w_hh, b_ih, b_hh, fc3_w, fc3_b, out_0, out_1, out_2
):
    nc = tc.nc
    with ExitStack() as ctx:
        ctx.enter_context(tc.manual_schedule())
        consts = ctx.enter_context(tc.tile_pool(name="consts", bufs=1))
        raw = ctx.enter_context(tc.tile_pool(name="raw", bufs=1))
        regroup = ctx.enter_context(tc.tile_pool(name="regroup", bufs=4))
        mx = ctx.enter_context(tc.tile_pool(name="mx", bufs=1))
        work = ctx.enter_context(tc.tile_pool(name="work", bufs=1))
        weight_banks = ctx.enter_context(tc.psum_pool(name="weight_banks", bufs=4))
        gate_banks = ctx.enter_context(tc.psum_pool(name="gate_banks", bufs=2))
        other_banks = ctx.enter_context(tc.psum_pool(name="other_banks", bufs=2))

        x_raw = raw.tile([P, 2 * K], BF16)
        b_rows = raw.tile([P, HIDDEN], BF16)
        cx_raw = raw.tile([P, HIDDEN], BF16)
        fc3_raw = raw.tile([P, K], BF16)
        w_raw = [raw.tile([P, BLOCKS * K], BF16, name="w_raw_%d" % c) for c in range(CHUNKS)]

        def load_x():
            nc.sync.dma_start(out=x_raw[:, 0:K], in_=h_fc2)
            nc.sync.dma_start(out=x_raw[:, K : 2 * K], in_=hx)

        def load_biases():
            nc.vector.memset(b_rows[:], 0.0)
            nc.sync.dma_start(out=b_rows[0:GATES, :], in_=b_ih.rearrange("(g h) -> g h", g=GATES))
            nc.sync.dma_start(out=b_rows[GATES : 2 * GATES, :], in_=b_hh.rearrange("(g h) -> g h", g=GATES))
            nc.sync.dma_start(
                out=b_rows[FC3_B_ROW : FC3_B_ROW + 1, 0:ACTIONS], in_=fc3_b.rearrange("(o a) -> o a", o=1)
            )

        def load_cx():
            nc.sync.dma_start(out=cx_raw[:], in_=cx)

        def load_fc3_w():
            nc.sync.dma_start(out=fc3_raw[:], in_=fc3_w)

        small_loads = {0: load_x, 3: load_biases, 5: load_cx, 7: load_fc3_w}
        def load_weights(c, halves):
            g, s = divmod(c, 2)
            rows = (w_ih, w_hh)[s][g * HIDDEN : (g + 1) * HIDDEN, :].rearrange("(p j) k -> p (j k)", j=BLOCKS)
            cols = slice(halves[0] * HALF_BLOCKS * K, (halves[-1] + 1) * HALF_BLOCKS * K)
            nc.sync.dma_start(out=w_raw[c][:, cols], in_=rows[:, cols])

        for step in range(CHUNKS):
            if step in SPLIT_STEPS:
                for c, half in step_halves(step):
                    load_weights(c, (half,))
            else:
                load_weights(step, (0, 1))
            if step in small_loads:
                small_loads[step]()

        ident = consts.tile([P, P], F32)
        make_identity(nc, ident[:])
        ident_bf16 = consts.tile([P, P], BF16)
        make_identity(nc, ident_bf16[:])
        warm = consts.tile([P, 1], F32)
        nc.vector.memset(warm[:], 0.0)
        nc.scalar.activation(out=warm[:], in_=warm[:], func=FUNC.Sigmoid)

        x_codes = mx.tile([P, 2 * BATCH], U32, align_bytes=64)
        x_scales = mx.tile([P, 2 * BATCH], U8, align_bytes=64)

        in_psum = {}
        x_grouped = work.tile([P, 2 * BATCH * PACK], BF16, align_bytes=64)

        def transpose_x():
            in_psum["x"] = other_banks.tile([P, SLOTS, P], F32, tag="other", name="x_bank")
            transpose_four(nc, in_psum["x"], x_raw[:].bitcast(F32), ident[:])

        def empty_x():
            copy_pairs_side_by_side(nc.scalar.copy, x_grouped, in_psum["x"])

        def quantise_x():
            nc.vector.quantize_mx(out=x_codes[:].bitcast(FP8X4), scales=x_scales[:], in_=x_grouped[:])

        bias = work.tile([P, BLOCKS, GATES], F32)
        fc3_b_rows = work.tile([P, ACTIONS], F32)

        def transpose_biases():
            in_psum["b"] = other_banks.tile([P, BLOCKS, P], BF16, tag="other", name="b_t")
            b_blocks = b_rows[:].rearrange("r (p j) -> r j p", j=BLOCKS)
            for j in range(BLOCKS):
                nc.tensor.transpose(in_psum["b"][:, j, :], b_blocks[:, j, :], ident_bf16[:])

        def spread_fc3_b():
            in_psum["fc3_b"] = other_banks.tile([P, ACTIONS], F32, tag="other", name="fc3_b_bank")
            nc.tensor.matmul(
                out=in_psum["fc3_b"][:],
                lhsT=ident_bf16[:, FC3_B_ROW : FC3_B_ROW + 1].to_broadcast([P, P]),
                rhs=b_rows[:, 0:ACTIONS],
                start=True,
                stop=True,
            )

        b_cols = work.tile([P, BLOCKS, 2 * GATES], F32)

        def add_biases():
            nc.vector.tensor_copy(out=b_cols[:], in_=in_psum["b"][:, :, 0 : 2 * GATES])
            nc.vector.tensor_copy(out=fc3_b_rows[:], in_=in_psum["fc3_b"][:])
            nc.vector.tensor_add(out=bias[:], in0=b_cols[:, :, 0:GATES], in1=b_cols[:, :, GATES : 2 * GATES])

        def transpose_cx():
            in_psum["cx_t"] = other_banks.tile([P, BLOCKS, BATCH], BF16, tag="other", name="cx_t")
            cx_blocks = cx_raw[:].rearrange("b (p j) -> b j p", j=BLOCKS)
            for j in range(BLOCKS):
                nc.tensor.transpose(in_psum["cx_t"][:, j, :], cx_blocks[:, j, :], ident_bf16[:])

        fc3_codes = mx.tile([P, ACTIONS], U32, align_bytes=64)
        fc3_scales = mx.tile([P, ACTIONS], U8, align_bytes=64)

        fc3_grouped = work.tile([P, ACTIONS * PACK], BF16, align_bytes=64)

        def transpose_fc3_w():
            in_psum["fc3"] = other_banks.tile([P, 2, P], F32, tag="other", name="fc3_bank")
            fc3_words = fc3_raw[:].bitcast(F32).rearrange("a (p u) -> a u p", u=2)
            for u in range(2):
                nc.tensor.transpose(in_psum["fc3"][:, u, :], fc3_words[:, u, :], ident[:])

        def empty_fc3_w():
            nc.scalar.copy(
                out=fc3_grouped[:].bitcast(F32).rearrange("p (a u) -> p a u", u=2),
                in_=in_psum["fc3"][:].rearrange("p u a -> p a u"),
            )

        def quantise_fc3_w():
            nc.vector.quantize_mx(out=fc3_codes[:].bitcast(FP8X4), scales=fc3_scales[:], in_=fc3_grouped[:])

        w_codes = [mx.tile([P, BLOCKS * P], U32, align_bytes=64, name="w_codes_%d" % c) for c in range(CHUNKS)]
        w_scales = [mx.tile([P, BLOCKS * P], U8, align_bytes=64, name="w_scales_%d" % c) for c in range(CHUNKS)]
        grouped = {}

        bank_of = {}

        def transpose(c, half):
            words = w_raw[c][:].bitcast(F32)
            bank_of[c, half] = weight_banks.tile([P, SLOTS, P], F32, tag="weights", name="bank_%d_%d" % (c, half))
            transpose_four(nc, bank_of[c, half], words[:, half * SLOTS * P : (half + 1) * SLOTS * P], ident[:])

        def empty(copy, c, half):
            grouped[c, half] = regroup.tile(
                [P, HALF_BLOCKS * P * PACK], BF16, align_bytes=64, tag="grouped", name="grouped_%d_%d" % (c, half)
            )
            copy_pairs_side_by_side(copy, grouped[c, half], bank_of[c, half])

        def quantise(c, half):
            cols = slice(half * HALF_BLOCKS * P, (half + 1) * HALF_BLOCKS * P)
            nc.vector.quantize_mx(
                out=w_codes[c][:, cols].bitcast(FP8X4), scales=w_scales[c][:, cols], in_=grouped[c, half][:]
            )

        gate = [work.tile([P, BLOCKS, BATCH], F32, name="gate_%d" % g) for g in range(GATES)]

        gate_bank_of = {}

        def multiply(g, half):
            gate_bank = gate_banks.tile([P, HALF_BLOCKS, BATCH], F32, tag="gate")
            gate_bank_of[g, half] = gate_bank
            for i in range(HALF_BLOCKS):
                j = half * HALF_BLOCKS + i
                for s in range(2):
                    nc.tensor.matmul_mx(
                        out=gate_bank[:, i, :],
                        lhsT=w_codes[2 * g + s][:, j * P : (j + 1) * P].bitcast(FP8X4),
                        lhsT_scale=w_scales[2 * g + s][:, j * P : (j + 1) * P],
                        rhs=x_codes[:, s * BATCH : (s + 1) * BATCH].bitcast(FP8X4),
                        rhs_scale=x_scales[:, s * BATCH : (s + 1) * BATCH],
                        start=(s == 0),
                        stop=(s == 1),
                    )

        def activate(g, half):
            for i in range(HALF_BLOCKS):
                j = half * HALF_BLOCKS + i
                nc.scalar.activation(
                    out=gate[g][:, j, :],
                    in_=gate_bank_of[g, half][:, i, :],
                    func=FUNC.Tanh if g == GATE_G else FUNC.Sigmoid,
                    bias=bias[:, j, g : g + 1],
                )

        kept = work.tile([P, BLOCKS, BATCH], F32)
        fresh = work.tile([P, BLOCKS, BATCH], F32)
        cx_new = work.tile([P, BLOCKS, BATCH], F32)
        tanh_c = work.tile([P, BLOCKS, BATCH], F32)
        hx_grouped = work.tile([P, BATCH, PACK], BF16, align_bytes=64)

        def of_half(value, half):
            return value[:, half * HALF_BLOCKS : (half + 1) * HALF_BLOCKS, :]

        def keep_cell(half):
            nc.vector.tensor_mul(
                out=of_half(kept, half), in0=of_half(gate[GATE_F], half), in1=of_half(in_psum["cx_t"], half)
            )

        def new_cell(half):
            nc.vector.tensor_mul(
                out=of_half(fresh, half), in0=of_half(gate[GATE_I], half), in1=of_half(gate[GATE_G], half)
            )

        def add_cell(half):
            nc.vector.tensor_add(out=of_half(cx_new, half), in0=of_half(kept, half), in1=of_half(fresh, half))

        def tanh_cell(half):
            nc.scalar.activation(out=of_half(tanh_c, half), in_=of_half(cx_new, half), func=FUNC.Tanh)

        def round_hx(half):
            nc.vector.tensor_mul(
                out=hx_grouped[:, :, half * HALF_BLOCKS : (half + 1) * HALF_BLOCKS],
                in0=of_half(gate[GATE_O], half).rearrange("p j b -> p b j"),
                in1=of_half(tanh_c, half).rearrange("p j b -> p b j"),
            )

        def turn(value_t, label):
            bank = weight_banks.tile([P, SLOTS, P], F32, tag="weights", name="bank_" + label)
            for j in range(BLOCKS):
                nc.tensor.transpose(bank[:, j, :], value_t[:, j, :], ident[:])
            in_psum[label] = bank[:].rearrange("b j p -> b p j")

        def by_unit(rows):
            return rows[:].rearrange("b (p j) -> b p j", j=BLOCKS)

        cx_rows = work.tile([P, HIDDEN], F32)
        tanh_rows = work.tile([P, HIDDEN], F32)
        hx_rows = work.tile([P, HIDDEN], F32)
        hx_codes = mx.tile([P, BATCH], U32, align_bytes=64)
        hx_scales = mx.tile([P, BATCH], U8, align_bytes=64)
        act = work.tile([P, ACTIONS], F32)

        def quantise_hx():
            nc.vector.quantize_mx(
                out=hx_codes[:].bitcast(FP8X4),
                scales=hx_scales[:],
                in_=hx_grouped[:].rearrange("p b j -> p (b j)"),
            )

        def multiply_head():
            in_psum["act"] = gate_banks.tile([P, ACTIONS], F32, tag="gate", name="act_bank")
            nc.tensor.matmul_mx(
                out=in_psum["act"][:],
                lhsT=hx_codes[:].bitcast(FP8X4),
                lhsT_scale=hx_scales[:],
                rhs=fc3_codes[:].bitcast(FP8X4),
                rhs_scale=fc3_scales[:],
                start=True,
                stop=True,
            )

        vec, sca = nc.vector.tensor_copy, nc.scalar.copy

        for step in range(CHUNKS):
            (c0, h0), (c1, h1) = step_halves(step)
            if step == 6:
                transpose_cx()
            transpose(c0, h0)
            transpose(c1, h1)
            if step == 0:
                transpose_x()
            if step == 3:
                transpose_biases()
                spread_fc3_b()
            if step >= 1:
                for c, h in step_halves(step - 1):
                    quantise(c, h)
            if step == 6:
                keep_cell(0)
            if step == 6:
                keep_cell(1)
            if step == 1:
                empty_x()
            if step == 2:
                quantise_x()
            gate_done = (step - 3) // 2
            if step >= 3 and (step - 3) % 2 == 0:
                multiply(gate_done, 0)
                multiply(gate_done, 1)
            empty(sca, c0, h0)
            empty(vec if step in VECTOR_STEPS else sca, c1, h1)
            if step == 3:
                add_biases()
            if step >= 3 and (step - 3) % 2 == 0:
                activate(gate_done, 0)
                activate(gate_done, 1)

        transpose_fc3_w()
        quantise(CHUNKS - 2, 1)
        quantise(CHUNKS - 1, 1)
        empty_fc3_w()
        multiply(GATE_O, 0)
        multiply(GATE_O, 1)
        new_cell(0)
        new_cell(1)
        activate(GATE_O, 0)
        activate(GATE_O, 1)
        add_cell(0)
        add_cell(1)
        tanh_cell(0)
        tanh_cell(1)
        quantise_fc3_w()
        turn(cx_new, "tanh")
        turn(cx_new, "cx")
        turn(gate[GATE_O], "o")
        nc.scalar.activation(out=by_unit(tanh_rows), in_=in_psum["tanh"], func=FUNC.Tanh)
        nc.scalar.copy(out=by_unit(cx_rows)[:, 64:, :], in_=in_psum["tanh"][:, 64:, :])
        round_hx(0)
        round_hx(1)
        nc.vector.tensor_copy(out=by_unit(cx_rows)[:, 0:64, :], in_=in_psum["cx"][:, 0:64, :])
        nc.sync.dma_start(out=out_2, in_=cx_rows[:])
        quantise_hx()
        multiply_head()
        nc.vector.tensor_mul(out=by_unit(hx_rows), in0=in_psum["o"], in1=by_unit(tanh_rows))
        nc.sync.dma_start(out=out_1, in_=hx_rows[:])
        nc.vector.tensor_add(out=act[:], in0=in_psum["act"][:], in1=fc3_b_rows[:])
        nc.scalar.activation(out=act[:], in_=act[:], func=FUNC.Tanh)
        nc.sync.dma_start(out=out_0, in_=act[:])
